import numpy as np
import ml_dtypes


def mxq(x, axis, fmt="e4m3"):
    dtype, down = {"e4m3": (ml_dtypes.float8_e4m3fn, 7), "e5m2": (ml_dtypes.float8_e5m2, 14)}[fmt]
    v = np.moveaxis(np.asarray(x, np.float32).astype(ml_dtypes.bfloat16).astype(np.float64), axis, -1)
    blocks = v.reshape(v.shape[:-1] + (-1, 32))
    amax = np.abs(blocks).max(-1, keepdims=True)
    byte = np.maximum(np.where(amax > 0, np.frexp(amax)[1] - 1 + 127, 0) - down, 1)
    scale = np.exp2(byte - 127.0)
    codes = (blocks / scale).astype(np.float32).astype(dtype).astype(np.float64)
    return np.moveaxis((codes * scale).reshape(v.shape), -1, axis)


WIDE = False


def mx_kscale(k):
    if not WIDE:
        return np.ones(k)
    levels = np.array([10, -10, 5, -5, 0])
    a = np.random.permutation(np.resize(levels, k // 512 * 4)).reshape(k // 512, 4)
    idx = np.arange(k)
    return np.exp2(a[idx // 512, idx % 128 // 32])


BF16 = ml_dtypes.bfloat16


def bf(x):
    return np.asarray(x, np.float32).astype(BF16)


def f64(x):
    return np.asarray(x).astype(np.float64)


B, S, H, D = 2, 256, 4, 512
GAMMA = 64.0


def squash(v):
    return v / (1.0 + np.abs(v))


def setup_inputs():
    s = mx_kscale(D)
    return {"hq1": bf(np.random.standard_normal((B, H, S, D)) * 0.25 * s),
            "hk1": bf(np.random.standard_normal((B, H, S, D)) * 0.25 * s),
            "proj1": bf(np.random.standard_normal((1, H, D, D)) * 0.75 / np.sqrt(D) / s[:, None]),
            "bias1": bf(np.random.standard_normal((1, H, 1, D)) * 0.1)}


def reference(hq1, hk1, proj1, bias1):
    pq = mxq(f64(proj1), 2, "e4m3")
    hq = ((mxq(f64(hq1), 3, "e4m3") @ pq) + f64(bias1)) + f64(hq1)
    hk = ((mxq(f64(hk1), 3, "e4m3") @ pq) + f64(bias1)) + f64(hk1)
    qh = squash(hq * GAMMA)
    kh = squash(hk * GAMMA)
    return mxq(qh, 3, "e4m3") @ mxq(kh, 3, "e4m3").transpose(0, 1, 3, 2)

@@ -1,0 +1,298 @@
+from contextlib import ExitStack
+
+import concourse.mybir as mybir
+from concourse.masks import make_identity
+
+BF16 = mybir.dt.bfloat16
+F32 = mybir.dt.float32
+U32 = mybir.dt.uint32
+U8 = mybir.dt.uint8
+FP8X4 = mybir.dt.float8_e4m3fn_x4
+ACT = mybir.ActivationFunctionType
+ALU = mybir.AluOpType
+
+P = 128
+PACK = 4
+BATCH = 2
+HEADS = 4
+SEQ = 256
+WIDTH = 512
+GAMMA = 64.0
+TOKEN_TILES = SEQ // P
+FEATURE_TILES = WIDTH // P
+SIDES = 2
+UNITS = HEADS * BATCH * SIDES
+UNITS_PER_HEAD = BATCH * SIDES
+RUN = 4
+FIRST_STEP = -5
+BIAS_STEP = -2
+
+FLOPS = 2 * UNITS * SEQ * WIDTH * WIDTH + 2 * HEADS * BATCH * SEQ * SEQ * WIDTH
+
+
+def tile_decoder_pb_kernel(tc, hq1, hk1, proj1, bias1, out):
+    nc = tc.nc
+    assert FEATURE_TILES == PACK
+
+    def place(unit):
+        return unit // UNITS_PER_HEAD, (unit // SIDES) % BATCH, unit % SIDES
+
+    def live(unit):
+        return 0 <= unit < UNITS
+
+    with ExitStack() as ctx:
+        consts = ctx.enter_context(tc.tile_pool(name="consts", bufs=1))
+        inputs = ctx.enter_context(tc.tile_pool(name="inputs", bufs=1))
+        pairs = ctx.enter_context(tc.tile_pool(name="pairs", bufs=2))
+        quads = ctx.enter_context(tc.tile_pool(name="quads", bufs=4))
+        psum_t = ctx.enter_context(tc.psum_pool(name="psum_t", bufs=2))
+        psum_h = ctx.enter_context(tc.psum_pool(name="psum_h", bufs=4))
+        psum_o = ctx.enter_context(tc.psum_pool(name="psum_o", bufs=2))
+        ctx.enter_context(tc.manual_schedule())
+
+        x_rows, w_rows = {}, {}
+        x_t, grouped_x, x_codes, x_scales = {}, {}, {}, {}
+        grouped_w, w_codes, w_scales = {}, {}, {}
+        acc, hidden, magnitude, root, shrink = {}, {}, {}, {}, {}
+        grouped_h, h_codes, h_scales = {}, {}, {}
+        scores_ps = {}
+
+        identity = consts.tile([P, P], BF16)
+        make_identity(nc, identity[:])
+        bias_rows = consts.tile([P, P], BF16)
+        nc.vector.memset(bias_rows[:], 0.0)
+        one = consts.tile([P, 1], F32)
+        nc.vector.memset(one[:], 1.0)
+
+        def load_x(unit):
+            head, batch, side = place(unit)
+            source = (hq1, hk1)[side]
+            rows = inputs.tile([P, TOKEN_TILES, WIDTH], BF16, name="x_rows%d" % unit)
+            nc.sync.dma_start(
+                out=rows[:], in_=source[batch, head].rearrange("(a p) k -> p a k", p=P)
+            )
+            x_rows[unit] = rows
+
+        def load_w(head):
+            rows = inputs.tile([P, PACK, WIDTH], BF16, name="w_rows%d" % head)
+            nc.sync.dma_start(
+                out=rows[:], in_=proj1[0, head].rearrange("(t p) n -> p t n", p=P)
+            )
+            w_rows[head] = rows
+
+        for head in range(HEADS):
+            first = head * UNITS_PER_HEAD
+            load_x(first)
+            load_w(head)
+            for unit in range(first + 1, first + UNITS_PER_HEAD):
+                load_x(unit)
+
+        nc.scalar.dma_start(
+            out=bias_rows[0 : HEADS * FEATURE_TILES, :],
+            in_=bias1.rearrange("o h i (m p) -> (o h i m) p", p=P),
+        )
+        bias = consts.tile([P, HEADS * FEATURE_TILES], F32)
+
+        def turn_bias():
+            bias_t = psum_o.tile([P, P], BF16, tag="product")
+            nc.tensor.transpose(out=bias_t[:], in_=bias_rows[:], identity=identity[:])
+            nc.vector.tensor_copy(out=bias[:], in_=bias_t[:, 0 : HEADS * FEATURE_TILES])
+
+        warm = consts.tile([P, 1], F32)
+        nc.scalar.activation(out=warm[:], in_=one[:], func=ACT.Abs_reciprocal_sqrt)
+
+        def regroup_w(head):
+            if not 0 <= head < HEADS:
+                return
+            grouped = pairs.tile([P, WIDTH, PACK], BF16, align_bytes=64, name="grouped_w")
+            nc.vector.tensor_copy(
+                out=grouped[:].rearrange("p (c i) t -> p c t i", i=RUN),
+                in_=w_rows[head][:].rearrange("p t (c i) -> p c t i", i=RUN),
+            )
+            grouped_w[head] = grouped
+
+        def quantise_w(head):
+            if not 0 <= head < HEADS:
+                return
+            codes = pairs.tile([P, WIDTH], U32, align_bytes=64, name="w_codes")
+            scales = pairs.tile([P, WIDTH], U8, align_bytes=64, name="w_scales")
+            nc.vector.quantize_mx(
+                out=codes[:].bitcast(FP8X4),
+                scales=scales[:],
+                in_=grouped_w[head][:].rearrange("p n t -> p (n t)"),
+            )
+            w_codes[head], w_scales[head] = codes, scales
+
+        def transpose_x(unit):
+            if not live(unit):
+                return
+            turned = psum_t.tile([P, TOKEN_TILES, PACK, P], BF16, name="turned")
+            for a in range(TOKEN_TILES):
+                for t in range(PACK):
+                    nc.tensor.transpose(
+                        out=turned[:, a, t, :],
+                        in_=x_rows[unit][:, a, t * P : (t + 1) * P],
+                        identity=identity[:],
+                    )
+            x_t[unit] = turned
+
+        def regroup_x(unit):
+            if not live(unit):
+                return
+            grouped = quads.tile([P, SEQ, PACK], BF16, align_bytes=64, name="grouped_x")
+            target = grouped[:].rearrange("p (a r) t -> p a r t", a=TOKEN_TILES)
+            origin = x_t[unit][:].rearrange("p a t r -> p a r t")
+            if unit % 2 == 0:
+                nc.scalar.copy(out=target, in_=origin)
+            else:
+                nc.vector.tensor_copy(out=target, in_=origin)
+            grouped_x[unit] = grouped
+
+        def quantise_x(unit):
+            if not live(unit):
+                return
+            codes = pairs.tile([P, SEQ], U32, align_bytes=64, name="x_codes")
+            scales = pairs.tile([P, SEQ], U8, align_bytes=64, name="x_scales")
+            nc.vector.quantize_mx(
+                out=codes[:].bitcast(FP8X4),
+                scales=scales[:],
+                in_=grouped_x[unit][:].rearrange("p s t -> p (s t)"),
+            )
+            x_codes[unit], x_scales[unit] = codes, scales
+
+        def project(unit):
+            if not live(unit):
+                return
+            head = place(unit)[0]
+            acc[unit] = []
+            for bank in range(FEATURE_TILES // 2):
+                sums = psum_h.tile([P, 2, SEQ], F32, name="sums")
+                for j in range(2):
+                    cols = slice((2 * bank + j) * P, (2 * bank + j + 1) * P)
+                    nc.tensor.matmul_mx(
+                        out=sums[:, j, :],
+                        lhsT=w_codes[head][:, cols].bitcast(FP8X4),
+                        lhsT_scale=w_scales[head][:, cols],
+                        rhs=x_codes[unit][:].bitcast(FP8X4),
+                        rhs_scale=x_scales[unit][:],
+                        start=True,
+                        stop=True,
+                    )
+                    acc[unit].append(sums[:, j, :])
+
+        def add_bias_and_residual(unit):
+            if not live(unit):
+                return
+            head = place(unit)[0]
+            h = quads.tile([P, FEATURE_TILES, SEQ], F32, name="hidden")
+            for m in range(FEATURE_TILES):
+                column = head * FEATURE_TILES + m
+                nc.vector.scalar_tensor_tensor(
+                    out=h[:, m, :],
+                    in0=acc[unit][m],
+                    scalar=bias[:, column : column + 1],
+                    in1=grouped_x[unit][:, :, m],
+                    op0=ALU.add,
+                    op1=ALU.add,
+                )
+            hidden[unit] = h
+
+        def take_magnitude(unit):
+            if not live(unit):
+                return
+            a = pairs.tile([P, FEATURE_TILES, SEQ], F32, name="magnitude")
+            nc.scalar.activation(out=a[:], in_=hidden[unit][:], func=ACT.Abs)
+            magnitude[unit] = a
+
+        def take_root(unit):
+            if not live(unit):
+                return
+            r = pairs.tile([P, FEATURE_TILES, SEQ], F32, name="root")
+            nc.scalar.activation(
+                out=r[:],
+                in_=magnitude[unit][:],
+                func=ACT.Abs_reciprocal_sqrt,
+                scale=GAMMA,
+                bias=one[:, 0:1],
+            )
+            root[unit] = r
+
+        def take_shrink(unit):
+            if not live(unit):
+                return
+            s = pairs.tile([P, FEATURE_TILES, SEQ], F32, name="shrink")
+            nc.scalar.activation(out=s[:], in_=root[unit][:], func=ACT.Square, scale=GAMMA**0.5)
+            shrink[unit] = s
+
+        def squash(unit):
+            if not live(unit):
+                return
+            grouped = pairs.tile([P, SEQ, PACK], BF16, align_bytes=64, name="grouped_h")
+            nc.vector.tensor_tensor(
+                out=grouped[:].rearrange("p (c i) t -> p c t i", i=RUN),
+                in0=hidden[unit][:].rearrange("p t (c i) -> p c t i", i=RUN),
+                in1=shrink[unit][:].rearrange("p t (c i) -> p c t i", i=RUN),
+                op=ALU.mult,
+            )
+            grouped_h[unit] = grouped
+
+        def quantise_h(unit):
+            if not live(unit):
+                return
+            side = place(unit)[2]
+            codes = pairs.tile([P, SEQ], U32, align_bytes=64, name="h_codes%d" % side)
+            scales = pairs.tile([P, SEQ], U8, align_bytes=64, name="h_scales%d" % side)
+            nc.vector.quantize_mx(
+                out=codes[:].bitcast(FP8X4),
+                scales=scales[:],
+                in_=grouped_h[unit][:].rearrange("p s t -> p (s t)"),
+            )
+            h_codes[unit], h_scales[unit] = codes, scales
+
+        def score(key_unit):
+            if not live(key_unit) or place(key_unit)[2] == 0:
+                return
+            query_unit = key_unit - 1
+            product = psum_o.tile([P, TOKEN_TILES, SEQ], F32, name="product")
+            for a in range(TOKEN_TILES):
+                cols = slice(a * P, (a + 1) * P)
+                nc.tensor.matmul_mx(
+                    out=product[:, a, :],
+                    lhsT=h_codes[query_unit][:, cols].bitcast(FP8X4),
+                    lhsT_scale=h_scales[query_unit][:, cols],
+                    rhs=h_codes[key_unit][:].bitcast(FP8X4),
+                    rhs_scale=h_scales[key_unit][:],
+                    start=True,
+                    stop=True,
+                )
+            scores_ps[key_unit] = product
+
+        def store(key_unit):
+            if not live(key_unit) or place(key_unit)[2] == 0:
+                return
+            head, batch = place(key_unit)[0:2]
+            result = pairs.tile([P, TOKEN_TILES, SEQ], F32, name="result")
+            nc.scalar.copy(out=result[:], in_=scores_ps[key_unit][:])
+            nc.sync.dma_start(
+                out=out[batch, head].rearrange("(a p) t -> p a t", p=P), in_=result[:]
+            )
+
+        for i in range(FIRST_STEP, UNITS + 3):
+            transpose_x(i + 3)
+            if i == BIAS_STEP:
+                turn_bias()
+            squash(i - 2)
+            take_magnitude(i)
+            add_bias_and_residual(i + 1)
+            take_shrink(i - 1)
+            quantise_h(i - 2)
+            score(i - 2)
+            take_root(i)
+            quantise_x(i + 2)
+            project(i + 2)
+            regroup_x(i + 3)
+            if (i + 5) % UNITS_PER_HEAD == 0:
+                regroup_w((i + 5) // UNITS_PER_HEAD)
+            if (i + 3) % UNITS_PER_HEAD == 0:
+                quantise_w((i + 3) // UNITS_PER_HEAD)
+            store(i - 3)

@@ -20,6 +20,8 @@ WIDTH = 512
 GAMMA = 64.0
 TOKEN_TILES = SEQ // P
 FEATURE_TILES = WIDTH // P
+PAIR = 2
+HALVES = PACK // PAIR
 SIDES = 2
 UNITS = HEADS * BATCH * SIDES
 UNITS_PER_HEAD = BATCH * SIDES
@@ -57,9 +59,9 @@ def tile_decoder_pb_kernel(tc, hq1, hk1, proj1, bias1, out):
         grouped_h, h_codes, h_scales = {}, {}, {}
         scores_ps = {}
 
-        identity = consts.tile([P, P], BF16)
+        identity = consts.tile([P, P], F32)
         make_identity(nc, identity[:])
-        bias_rows = consts.tile([P, P], BF16)
+        bias_rows = consts.tile([P, PAIR * P], BF16)
         nc.vector.memset(bias_rows[:], 0.0)
         one = consts.tile([P, 1], F32)
         nc.vector.memset(one[:], 1.0)
@@ -76,27 +78,28 @@ def tile_decoder_pb_kernel(tc, hq1, hk1, proj1, bias1, out):
         def load_w(head):
             rows = inputs.tile([P, PACK, WIDTH], BF16, name="w_rows%d" % head)
             nc.sync.dma_start(
-                out=rows[:], in_=proj1[0, head].rearrange("(t p) n -> p t n", p=P)
+                out=rows[:].rearrange("p (u e) n -> p u e n", e=PAIR),
+                in_=proj1[0, head].rearrange("(u p e) n -> p u e n", p=P, e=PAIR),
             )
             w_rows[head] = rows
 
         for head in range(HEADS):
-            first = head * UNITS_PER_HEAD
-            load_x(first)
             load_w(head)
-            for unit in range(first + 1, first + UNITS_PER_HEAD):
+            for unit in range(head * UNITS_PER_HEAD, (head + 1) * UNITS_PER_HEAD):
                 load_x(unit)
 
         nc.scalar.dma_start(
-            out=bias_rows[0 : HEADS * FEATURE_TILES, :],
-            in_=bias1.rearrange("o h i (m p) -> (o h i m) p", p=P),
+            out=bias_rows[0 : HEADS * HALVES, :],
+            in_=bias1.rearrange("o h i (u w) -> (o h i u) w", u=HALVES),
         )
         bias = consts.tile([P, HEADS * FEATURE_TILES], F32)
 
         def turn_bias():
-            bias_t = psum_o.tile([P, P], BF16, tag="product")
-            nc.tensor.transpose(out=bias_t[:], in_=bias_rows[:], identity=identity[:])
-            nc.vector.tensor_copy(out=bias[:], in_=bias_t[:, 0 : HEADS * FEATURE_TILES])
+            bias_t = psum_o.tile([P, P], F32, tag="product")
+            nc.tensor.transpose(
+                out=bias_t[:], in_=bias_rows[:].bitcast(F32), identity=identity[:]
+            )
+            nc.vector.tensor_copy(out=bias[:], in_=bias_t[:, 0 : HEADS * HALVES].bitcast(BF16))
 
         warm = consts.tile([P, 1], F32)
         nc.scalar.activation(out=warm[:], in_=one[:], func=ACT.Abs_reciprocal_sqrt)
@@ -105,10 +108,16 @@ def tile_decoder_pb_kernel(tc, hq1, hk1, proj1, bias1, out):
             if not 0 <= head < HEADS:
                 return
             grouped = pairs.tile([P, WIDTH, PACK], BF16, align_bytes=64, name="grouped_w")
-            nc.vector.tensor_copy(
-                out=grouped[:].rearrange("p (c i) t -> p c t i", i=RUN),
-                in_=w_rows[head][:].rearrange("p t (c i) -> p c t i", i=RUN),
-            )
+            columns = w_rows[head][:].rearrange("p t (u q e) -> p t u q e", q=P, e=PAIR)
+            for m in range(FEATURE_TILES):
+                nc.vector.tensor_copy(
+                    out=grouped[:, m * P : (m + 1) * P, :].rearrange(
+                        "p (c i) t -> p c t i", i=RUN
+                    ),
+                    in_=columns[:, :, m // PAIR, :, m % PAIR].rearrange(
+                        "p t (c i) -> p c t i", i=RUN
+                    ),
+                )
             grouped_w[head] = grouped
 
         def quantise_w(head):
@@ -126,12 +135,13 @@ def tile_decoder_pb_kernel(tc, hq1, hk1, proj1, bias1, out):
         def transpose_x(unit):
             if not live(unit):
                 return
-            turned = psum_t.tile([P, TOKEN_TILES, PACK, P], BF16, name="turned")
+            turned = psum_t.tile([P, TOKEN_TILES, HALVES, P], F32, name="turned")
             for a in range(TOKEN_TILES):
-                for t in range(PACK):
+                words = x_rows[unit][:, a, :].bitcast(F32)
+                for u in range(HALVES):
                     nc.tensor.transpose(
-                        out=turned[:, a, t, :],
-                        in_=x_rows[unit][:, a, t * P : (t + 1) * P],
+                        out=turned[:, a, u, :],
+                        in_=words[:, u * P : (u + 1) * P],
                         identity=identity[:],
                     )
             x_t[unit] = turned
@@ -140,8 +150,13 @@ def tile_decoder_pb_kernel(tc, hq1, hk1, proj1, bias1, out):
             if not live(unit):
                 return
             grouped = quads.tile([P, SEQ, PACK], BF16, align_bytes=64, name="grouped_x")
-            target = grouped[:].rearrange("p (a r) t -> p a r t", a=TOKEN_TILES)
-            origin = x_t[unit][:].rearrange("p a t r -> p a r t")
+            target = (
+                grouped[:]
+                .rearrange("p s t -> p (s t)")
+                .bitcast(F32)
+                .rearrange("p (a r u) -> p a r u", a=TOKEN_TILES, u=HALVES)
+            )
+            origin = x_t[unit][:].rearrange("p a u r -> p a r u")
             if unit % 2 == 0:
                 nc.scalar.copy(out=target, in_=origin)
             else:
@@ -272,7 +287,7 @@ def tile_decoder_pb_kernel(tc, hq1, hk1, proj1, bias1, out):
                 return
             head, batch = place(key_unit)[0:2]
             result = pairs.tile([P, TOKEN_TILES, SEQ], F32, name="result")
-            nc.scalar.copy(out=result[:], in_=scores_ps[key_unit][:])
+            nc.vector.tensor_copy(out=result[:], in_=scores_ps[key_unit][:])
             nc.sync.dma_start(
                 out=out[batch, head].rearrange("(a p) t -> p a t", p=P), in_=result[:]
             )

@@ -26,15 +26,14 @@ SIDES = 2
 UNITS = HEADS * BATCH * SIDES
 UNITS_PER_HEAD = BATCH * SIDES
 RUN = 4
-FIRST_STEP = -5
-BIAS_STEP = -2
 
 FLOPS = 2 * UNITS * SEQ * WIDTH * WIDTH + 2 * HEADS * BATCH * SEQ * SEQ * WIDTH
 
 
+HALF = SEQ // 2
+
 def tile_decoder_pb_kernel(tc, hq1, hk1, proj1, bias1, out):
     nc = tc.nc
-    assert FEATURE_TILES == PACK
 
     def place(unit):
         return unit // UNITS_PER_HEAD, (unit // SIDES) % BATCH, unit % SIDES
@@ -47,11 +46,12 @@ def tile_decoder_pb_kernel(tc, hq1, hk1, proj1, bias1, out):
         inputs = ctx.enter_context(tc.tile_pool(name="inputs", bufs=1))
         pairs = ctx.enter_context(tc.tile_pool(name="pairs", bufs=2))
         quads = ctx.enter_context(tc.tile_pool(name="quads", bufs=4))
+        w_ring = ctx.enter_context(tc.tile_pool(name="w_ring", bufs=1))
+        wide = ctx.enter_context(tc.tile_pool(name="wide", bufs=4))
         psum_t = ctx.enter_context(tc.psum_pool(name="psum_t", bufs=2))
         psum_h = ctx.enter_context(tc.psum_pool(name="psum_h", bufs=4))
         psum_o = ctx.enter_context(tc.psum_pool(name="psum_o", bufs=2))
         ctx.enter_context(tc.manual_schedule())
-
         x_rows, w_rows = {}, {}
         x_t, grouped_x, x_codes, x_scales = {}, {}, {}, {}
         grouped_w, w_codes, w_scales = {}, {}, {}
@@ -59,34 +59,41 @@ def tile_decoder_pb_kernel(tc, hq1, hk1, proj1, bias1, out):
         grouped_h, h_codes, h_scales = {}, {}, {}
         scores_ps = {}
 
+        def load_x(unit):
+            head, batch, side = place(unit)
+            source = (hq1, hk1)[side]
+            rows = inputs.tile([P, TOKEN_TILES, WIDTH], BF16, name="x_rows%d" % unit)
+            nc.sync.dma_start(out=rows[:], in_=source[batch, head].rearrange("(a p) k -> p a k", p=P))
+            x_rows[unit] = rows
+
+        def load_w(head):
+            rows = inputs.tile([P, PACK, WIDTH], BF16, name="w_rows%d" % head)
+            w_rows[head] = rows
+            source = proj1[0, head].rearrange("(u p e) n -> p u e n", p=P, e=PAIR)
+            target = rows[:].rearrange("p (u e) n -> p u e n", e=PAIR)
+            if head > 0:
+                nc.sync.dma_start(out=target, in_=source)
+                return
+            for half in range(2):
+                cols = slice(half * PAIR * P, (half + 1) * PAIR * P)
+                for u in range(HALVES):
+                    nc.sync.dma_start(out=target[:, u, :, cols], in_=source[:, u, :, cols])
+
+        load_x(0)
+        load_w(0)
+        for unit in range(1, 4):
+            load_x(unit)
+        for head in range(1, HEADS):
+            load_w(head)
+            for unit in range(head * UNITS_PER_HEAD, (head + 1) * UNITS_PER_HEAD):
+                load_x(unit)
+
         identity = consts.tile([P, P], F32)
         make_identity(nc, identity[:])
         bias_rows = consts.tile([P, PAIR * P], BF16)
         nc.vector.memset(bias_rows[:], 0.0)
         one = consts.tile([P, 1], F32)
-        nc.vector.memset(one[:], 1.0)
-
-        def load_x(unit):
-            head, batch, side = place(unit)
-            source = (hq1, hk1)[side]
-            rows = inputs.tile([P, TOKEN_TILES, WIDTH], BF16, name="x_rows%d" % unit)
-            nc.sync.dma_start(
-                out=rows[:], in_=source[batch, head].rearrange("(a p) k -> p a k", p=P)
-            )
-            x_rows[unit] = rows
-
-        def load_w(head):
-            rows = inputs.tile([P, PACK, WIDTH], BF16, name="w_rows%d" % head)
-            nc.sync.dma_start(
-                out=rows[:].rearrange("p (u e) n -> p u e n", e=PAIR),
-                in_=proj1[0, head].rearrange("(u p e) n -> p u e n", p=P, e=PAIR),
-            )
-            w_rows[head] = rows
-
-        for head in range(HEADS):
-            load_w(head)
-            for unit in range(head * UNITS_PER_HEAD, (head + 1) * UNITS_PER_HEAD):
-                load_x(unit)
+        nc.vector.memset(one[:], 1.0 / GAMMA)
 
         nc.scalar.dma_start(
             out=bias_rows[0 : HEADS * HALVES, :],
@@ -96,41 +103,43 @@ def tile_decoder_pb_kernel(tc, hq1, hk1, proj1, bias1, out):
 
         def turn_bias():
             bias_t = psum_o.tile([P, P], F32, tag="product")
-            nc.tensor.transpose(
-                out=bias_t[:], in_=bias_rows[:].bitcast(F32), identity=identity[:]
-            )
+            nc.tensor.transpose(out=bias_t[:], in_=bias_rows[:].bitcast(F32), identity=identity[:])
+            return bias_t
+        def copy_bias(bias_t):
             nc.vector.tensor_copy(out=bias[:], in_=bias_t[:, 0 : HEADS * HALVES].bitcast(BF16))
 
         warm = consts.tile([P, 1], F32)
         nc.scalar.activation(out=warm[:], in_=one[:], func=ACT.Abs_reciprocal_sqrt)
 
-        def regroup_w(head):
-            if not 0 <= head < HEADS:
-                return
-            grouped = pairs.tile([P, WIDTH, PACK], BF16, align_bytes=64, name="grouped_w")
-            columns = w_rows[head][:].rearrange("p t (u q e) -> p t u q e", q=P, e=PAIR)
-            for m in range(FEATURE_TILES):
-                nc.vector.tensor_copy(
-                    out=grouped[:, m * P : (m + 1) * P, :].rearrange(
-                        "p (c i) t -> p c t i", i=RUN
-                    ),
-                    in_=columns[:, :, m // PAIR, :, m % PAIR].rearrange(
-                        "p t (c i) -> p c t i", i=RUN
-                    ),
-                )
-            grouped_w[head] = grouped
+        def make_w(head):
+            w_codes[head] = pairs.tile([P, WIDTH], U32, align_bytes=64, name="w_codes")
+            w_scales[head] = pairs.tile([P, WIDTH], U8, align_bytes=64, name="w_scales")
 
-        def quantise_w(head):
-            if not 0 <= head < HEADS:
-                return
-            codes = pairs.tile([P, WIDTH], U32, align_bytes=64, name="w_codes")
-            scales = pairs.tile([P, WIDTH], U8, align_bytes=64, name="w_scales")
+        def regroup_w(head, m, engine):
+            if head not in w_codes:
+                make_w(head)
+            grouped = (w_ring if engine == 'G' else wide).tile([P, P, PACK], BF16, align_bytes=64, name="grouped_w" + engine)
+            grouped_w[head, m] = grouped
+            columns = w_rows[head][:].rearrange("p t (u q e) -> p t u q e", q=P, e=PAIR)
+            src = columns[:, :, m // PAIR, :, m % PAIR]
+            dst = grouped[:]
+            if engine == 'G':
+                nc.gpsimd.tensor_scalar(out=dst, in0=src.rearrange("p t q -> p q t"), scalar1=1.0, scalar2=0.0, op0=ALU.mult, op1=ALU.add)
+            else:
+                o = dst.rearrange("p (c i) t -> p c t i", i=RUN)
+                s = src.rearrange("p t (c i) -> p c t i", i=RUN)
+                if engine == 'V':
+                    nc.vector.tensor_copy(out=o, in_=s)
+                else:
+                    nc.scalar.copy(out=o, in_=s)
+
+        def quantise_w(head, m):
+            cols = slice(m * P, (m + 1) * P)
             nc.vector.quantize_mx(
-                out=codes[:].bitcast(FP8X4),
-                scales=scales[:],
-                in_=grouped_w[head][:].rearrange("p n t -> p (n t)"),
+                out=w_codes[head][:, cols].bitcast(FP8X4),
+                scales=w_scales[head][:, cols],
+                in_=grouped_w[head, m][:].rearrange("p n t -> p (n t)"),
             )
-            w_codes[head], w_scales[head] = codes, scales
 
         def transpose_x(unit):
             if not live(unit):
@@ -139,25 +148,18 @@ def tile_decoder_pb_kernel(tc, hq1, hk1, proj1, bias1, out):
             for a in range(TOKEN_TILES):
                 words = x_rows[unit][:, a, :].bitcast(F32)
                 for u in range(HALVES):
-                    nc.tensor.transpose(
-                        out=turned[:, a, u, :],
-                        in_=words[:, u * P : (u + 1) * P],
-                        identity=identity[:],
-                    )
+                    nc.tensor.transpose(out=turned[:, a, u, :], in_=words[:, u * P : (u + 1) * P], identity=identity[:])
             x_t[unit] = turned
 
-        def regroup_x(unit):
+        def regroup_x(unit, want):
             if not live(unit):
                 return
+            if want != ('S' if unit % 2 == 0 else 'V'):
+                return
             grouped = quads.tile([P, SEQ, PACK], BF16, align_bytes=64, name="grouped_x")
-            target = (
-                grouped[:]
-                .rearrange("p s t -> p (s t)")
-                .bitcast(F32)
-                .rearrange("p (a r u) -> p a r u", a=TOKEN_TILES, u=HALVES)
-            )
+            target = grouped[:].rearrange("p s t -> p (s t)").bitcast(F32).rearrange("p (a r u) -> p a r u", a=TOKEN_TILES, u=HALVES)
             origin = x_t[unit][:].rearrange("p a u r -> p a r u")
-            if unit % 2 == 0:
+            if want == 'S':
                 nc.scalar.copy(out=target, in_=origin)
             else:
                 nc.vector.tensor_copy(out=target, in_=origin)
@@ -168,146 +170,200 @@ def tile_decoder_pb_kernel(tc, hq1, hk1, proj1, bias1, out):
                 return
             codes = pairs.tile([P, SEQ], U32, align_bytes=64, name="x_codes")
             scales = pairs.tile([P, SEQ], U8, align_bytes=64, name="x_scales")
-            nc.vector.quantize_mx(
-                out=codes[:].bitcast(FP8X4),
-                scales=scales[:],
-                in_=grouped_x[unit][:].rearrange("p s t -> p (s t)"),
-            )
+            nc.vector.quantize_mx(out=codes[:].bitcast(FP8X4), scales=scales[:], in_=grouped_x[unit][:].rearrange("p s t -> p (s t)"))
             x_codes[unit], x_scales[unit] = codes, scales
 
-        def project(unit):
+        def project(unit, ms=(0, 1, 2, 3)):
             if not live(unit):
                 return
             head = place(unit)[0]
-            acc[unit] = []
-            for bank in range(FEATURE_TILES // 2):
-                sums = psum_h.tile([P, 2, SEQ], F32, name="sums")
-                for j in range(2):
-                    cols = slice((2 * bank + j) * P, (2 * bank + j + 1) * P)
-                    nc.tensor.matmul_mx(
-                        out=sums[:, j, :],
-                        lhsT=w_codes[head][:, cols].bitcast(FP8X4),
-                        lhsT_scale=w_scales[head][:, cols],
-                        rhs=x_codes[unit][:].bitcast(FP8X4),
-                        rhs_scale=x_scales[unit][:],
-                        start=True,
-                        stop=True,
-                    )
-                    acc[unit].append(sums[:, j, :])
+            acc.setdefault(unit, {})
+            for m in ms:
+                if m % 2 == 0:
+                    acc[unit]['b'] = psum_h.tile([P, 2, SEQ], F32, name="sums")
+                sums = acc[unit]['b']
+                cols = slice(m * P, (m + 1) * P)
+                nc.tensor.matmul_mx(
+                    out=sums[:, m % 2, :],
+                    lhsT=w_codes[head][:, cols].bitcast(FP8X4),
+                    lhsT_scale=w_scales[head][:, cols],
+                    rhs=x_codes[unit][:].bitcast(FP8X4),
+                    rhs_scale=x_scales[unit][:],
+                    start=True,
+                    stop=True,
+                )
+                acc[unit][m] = sums[:, m % 2, :]
 
-        def add_bias_and_residual(unit):
+        def add(unit, ms=(0, 1, 2, 3), tok=slice(0, SEQ)):
             if not live(unit):
                 return
             head = place(unit)[0]
-            h = quads.tile([P, FEATURE_TILES, SEQ], F32, name="hidden")
-            for m in range(FEATURE_TILES):
+            if unit not in hidden:
+                hidden[unit] = quads.tile([P, FEATURE_TILES, SEQ], F32, name="hidden")
+                magnitude[unit] = pairs.tile([P, FEATURE_TILES, SEQ], F32, name="magnitude")
+                root[unit] = pairs.tile([P, FEATURE_TILES, SEQ], F32, name="root")
+                shrink[unit] = pairs.tile([P, FEATURE_TILES, SEQ], F32, name="shrink")
+            for m in ms:
                 column = head * FEATURE_TILES + m
                 nc.vector.scalar_tensor_tensor(
-                    out=h[:, m, :],
-                    in0=acc[unit][m],
+                    out=hidden[unit][:, m, tok],
+                    in0=acc[unit][m][:, tok],
                     scalar=bias[:, column : column + 1],
-                    in1=grouped_x[unit][:, :, m],
+                    in1=grouped_x[unit][:, tok, m],
                     op0=ALU.add,
                     op1=ALU.add,
                 )
-            hidden[unit] = h
 
-        def take_magnitude(unit):
+        def take_magnitude(unit, tok=slice(0, SEQ), ms=slice(0, 4)):
             if not live(unit):
                 return
-            a = pairs.tile([P, FEATURE_TILES, SEQ], F32, name="magnitude")
-            nc.scalar.activation(out=a[:], in_=hidden[unit][:], func=ACT.Abs)
-            magnitude[unit] = a
+            nc.scalar.activation(out=magnitude[unit][:, ms, tok], in_=hidden[unit][:, ms, tok], func=ACT.Abs)
 
-        def take_root(unit):
+        def take_root(unit, tok=slice(0, SEQ), ms=slice(0, 4)):
             if not live(unit):
                 return
-            r = pairs.tile([P, FEATURE_TILES, SEQ], F32, name="root")
-            nc.scalar.activation(
-                out=r[:],
-                in_=magnitude[unit][:],
-                func=ACT.Abs_reciprocal_sqrt,
-                scale=GAMMA,
-                bias=one[:, 0:1],
-            )
-            root[unit] = r
+            nc.scalar.activation(out=root[unit][:, ms, tok], in_=magnitude[unit][:, ms, tok], func=ACT.Abs_reciprocal_sqrt, bias=one[:, 0:1])
 
-        def take_shrink(unit):
+        def take_shrink(unit, tok=slice(0, SEQ), ms=slice(0, 4)):
             if not live(unit):
                 return
-            s = pairs.tile([P, FEATURE_TILES, SEQ], F32, name="shrink")
-            nc.scalar.activation(out=s[:], in_=root[unit][:], func=ACT.Square, scale=GAMMA**0.5)
-            shrink[unit] = s
+            nc.scalar.activation(out=shrink[unit][:, ms, tok], in_=root[unit][:, ms, tok], func=ACT.Square)
 
-        def squash(unit):
+        def squash(unit, tok=slice(0, SEQ)):
             if not live(unit):
                 return
-            grouped = pairs.tile([P, SEQ, PACK], BF16, align_bytes=64, name="grouped_h")
+            if unit not in grouped_h:
+                side = place(unit)[2]
+                grouped_h[unit] = pairs.tile([P, SEQ, PACK], BF16, align_bytes=64, name="grouped_h")
+                h_codes[unit] = pairs.tile([P, SEQ], U32, align_bytes=64, name="h_codes%d" % side)
+                h_scales[unit] = pairs.tile([P, SEQ], U8, align_bytes=64, name="h_scales%d" % side)
             nc.vector.tensor_tensor(
-                out=grouped[:].rearrange("p (c i) t -> p c t i", i=RUN),
-                in0=hidden[unit][:].rearrange("p t (c i) -> p c t i", i=RUN),
-                in1=shrink[unit][:].rearrange("p t (c i) -> p c t i", i=RUN),
+                out=grouped_h[unit][:, tok, :].rearrange("p (c i) t -> p c t i", i=RUN),
+                in0=hidden[unit][:, :, tok].rearrange("p t (c i) -> p c t i", i=RUN),
+                in1=shrink[unit][:, :, tok].rearrange("p t (c i) -> p c t i", i=RUN),
                 op=ALU.mult,
             )
-            grouped_h[unit] = grouped
 
-        def quantise_h(unit):
+        def quantise_h(unit, tok=slice(0, SEQ)):
             if not live(unit):
                 return
-            side = place(unit)[2]
-            codes = pairs.tile([P, SEQ], U32, align_bytes=64, name="h_codes%d" % side)
-            scales = pairs.tile([P, SEQ], U8, align_bytes=64, name="h_scales%d" % side)
             nc.vector.quantize_mx(
-                out=codes[:].bitcast(FP8X4),
-                scales=scales[:],
-                in_=grouped_h[unit][:].rearrange("p s t -> p (s t)"),
+                out=h_codes[unit][:, tok].bitcast(FP8X4),
+                scales=h_scales[unit][:, tok],
+                in_=grouped_h[unit][:, tok, :].rearrange("p s t -> p (s t)"),
             )
-            h_codes[unit], h_scales[unit] = codes, scales
 
-        def score(key_unit):
+        def score(key_unit, tok=slice(0, SEQ)):
             if not live(key_unit) or place(key_unit)[2] == 0:
                 return
             query_unit = key_unit - 1
-            product = psum_o.tile([P, TOKEN_TILES, SEQ], F32, name="product")
+            if tok.stop - tok.start == SEQ:
+                product = psum_o.tile([P, TOKEN_TILES, SEQ], F32, name="product")
+            else:
+                product = psum_o.tile([P, TOKEN_TILES, HALF], F32, name="product")
             for a in range(TOKEN_TILES):
                 cols = slice(a * P, (a + 1) * P)
                 nc.tensor.matmul_mx(
                     out=product[:, a, :],
                     lhsT=h_codes[query_unit][:, cols].bitcast(FP8X4),
                     lhsT_scale=h_scales[query_unit][:, cols],
-                    rhs=h_codes[key_unit][:].bitcast(FP8X4),
-                    rhs_scale=h_scales[key_unit][:],
+                    rhs=h_codes[key_unit][:, tok].bitcast(FP8X4),
+                    rhs_scale=h_scales[key_unit][:, tok],
                     start=True,
                     stop=True,
                 )
-            scores_ps[key_unit] = product
+            scores_ps[key_unit, tok.start] = product
 
-        def store(key_unit):
+        def store(key_unit, want, tok=slice(0, SEQ)):
             if not live(key_unit) or place(key_unit)[2] == 0:
+                return
+            if want != 'V':
                 return
             head, batch = place(key_unit)[0:2]
             result = pairs.tile([P, TOKEN_TILES, SEQ], F32, name="result")
-            nc.vector.tensor_copy(out=result[:], in_=scores_ps[key_unit][:])
-            nc.sync.dma_start(
-                out=out[batch, head].rearrange("(a p) t -> p a t", p=P), in_=result[:]
-            )
+            n = tok.stop - tok.start
+            nc.vector.tensor_copy(out=result[:, :, 0:n], in_=scores_ps[key_unit, tok.start][:])
+            nc.sync.dma_start(out=out[batch, head].rearrange("(a p) t -> p a t", p=P)[:, :, tok], in_=result[:, :, 0:n])
 
-        for i in range(FIRST_STEP, UNITS + 3):
-            transpose_x(i + 3)
-            if i == BIAS_STEP:
-                turn_bias()
-            squash(i - 2)
-            take_magnitude(i)
-            add_bias_and_residual(i + 1)
-            take_shrink(i - 1)
-            quantise_h(i - 2)
-            score(i - 2)
-            take_root(i)
-            quantise_x(i + 2)
-            project(i + 2)
-            regroup_x(i + 3)
-            if (i + 5) % UNITS_PER_HEAD == 0:
-                regroup_w((i + 5) // UNITS_PER_HEAD)
-            if (i + 3) % UNITS_PER_HEAD == 0:
-                quantise_w((i + 3) // UNITS_PER_HEAD)
-            store(i - 3)
+        W0S = (2,)
+        transpose_x(0)
+        bias_t = turn_bias()
+        regroup_x(0, 'S')
+        regroup_w(0, 0, 'V')
+        regroup_w(0, 1, 'V')
+        for m in W0S:
+            regroup_w(0, m, 'S')
+        quantise_x(0)
+        quantise_w(0, 0)
+        quantise_w(0, 1)
+        project(0, (0, 1))
+        transpose_x(1)
+        copy_bias(bias_t)
+        for m in (2, 3):
+            if m not in W0S:
+                regroup_w(0, m, 'V')
+        add(0, (0, 1))
+        take_magnitude(0, ms=slice(0, 2))
+        quantise_w(0, 2)
+        quantise_w(0, 3)
+        project(0, (2, 3))
+        transpose_x(2)
+        regroup_x(1, 'V')
+        regroup_x(1, 'S')
+        add(0, (2, 3))
+        take_magnitude(0, ms=slice(2, 4))
+        quantise_x(1)
+        project(1)
+        regroup_x(2, 'S')
+        regroup_x(2, 'V')
+        for i in range(0, UNITS + 3):
+            if i < UNITS - 1:
+                transpose_x(i + 3)
+                squash(i - 2)
+                if i > 0:
+                    take_magnitude(i)
+                if 2 < i < 11:
+                    quantise_w((i + 5) // 4, (i + 1) % 4)
+                if 1 < i < 10:
+                    regroup_w((i + 6) // 4, (i + 2) % 4, 'G')
+                add(i + 1)
+                take_shrink(i - 1)
+                if 0 <= i < 2:
+                    regroup_w(1, 2 * i, 'V')
+                    regroup_w(1, 2 * i + 1, 'V')
+                quantise_h(i - 2)
+                score(i - 2)
+                take_root(i)
+                if 1 <= i < 3:
+                    quantise_w(1, 2 * i - 2)
+                    quantise_w(1, 2 * i - 1)
+                quantise_x(i + 2)
+                project(i + 2)
+                regroup_x(i + 3, 'S')
+                regroup_x(i + 3, 'V')
+                store(i - 3, 'V')
+                store(i - 3, 'S')
+            elif i == UNITS - 1:
+                a, b = slice(0, HALF), slice(HALF, SEQ)
+                squash(i - 2)
+                take_magnitude(i, a)
+                take_shrink(i - 1)
+                take_root(i, a)
+                take_magnitude(i, b)
+                quantise_h(i - 2)
+                score(i - 2)
+                store(i - 3, 'V')
+                store(i - 3, 'S')
+                take_shrink(i, a)
+                squash(i - 1)
+                take_root(i, b)
+                quantise_h(i - 1)
+                store(i - 2, 'V')
+                store(i - 2, 'S')
+                take_shrink(i, b)
+                for t in (a, b):
+                    squash(i, t)
+                    quantise_h(i, t)
+                    score(i, t)
+                    store(i, 'V', t)
+                    store(i, 'S', t)

@@ -23,48 +23,44 @@ FEATURE_TILES = WIDTH // P
 PAIR = 2
 HALVES = PACK // PAIR
 SIDES = 2
-UNITS = HEADS * BATCH * SIDES
-UNITS_PER_HEAD = BATCH * SIDES
-RUN = 4
+TOKENS = SIDES * SEQ
+PAIRS = HEADS * BATCH
+HALF_WIDTH = WIDTH // HALVES
+COPY_RUN = 4
+WORD_RUN = 4
 
-FLOPS = 2 * UNITS * SEQ * WIDTH * WIDTH + 2 * HEADS * BATCH * SEQ * SEQ * WIDTH
-
-
-HALF = SEQ // 2
+FLOPS = 2 * PAIRS * TOKENS * WIDTH * WIDTH + 2 * PAIRS * SEQ * SEQ * WIDTH
 
 def tile_decoder_pb_kernel(tc, hq1, hk1, proj1, bias1, out):
     nc = tc.nc
 
-    def place(unit):
-        return unit // UNITS_PER_HEAD, (unit // SIDES) % BATCH, unit % SIDES
-
-    def live(unit):
-        return 0 <= unit < UNITS
-
     with ExitStack() as ctx:
         consts = ctx.enter_context(tc.tile_pool(name="consts", bufs=1))
         inputs = ctx.enter_context(tc.tile_pool(name="inputs", bufs=1))
-        pairs = ctx.enter_context(tc.tile_pool(name="pairs", bufs=2))
-        quads = ctx.enter_context(tc.tile_pool(name="quads", bufs=4))
-        w_ring = ctx.enter_context(tc.tile_pool(name="w_ring", bufs=1))
-        wide = ctx.enter_context(tc.tile_pool(name="wide", bufs=4))
+        ring = ctx.enter_context(tc.tile_pool(name="ring", bufs=1))
+        deep2 = ctx.enter_context(tc.tile_pool(name="deep2", bufs=2))
+        deep3 = ctx.enter_context(tc.tile_pool(name="deep3", bufs=3))
         psum_t = ctx.enter_context(tc.psum_pool(name="psum_t", bufs=2))
         psum_h = ctx.enter_context(tc.psum_pool(name="psum_h", bufs=4))
         psum_o = ctx.enter_context(tc.psum_pool(name="psum_o", bufs=2))
         ctx.enter_context(tc.manual_schedule())
-        x_rows, w_rows = {}, {}
-        x_t, grouped_x, x_codes, x_scales = {}, {}, {}, {}
+        x_rows, w_rows, turned_x = {}, {}, {}
+        grouped_x, x_codes, x_scales = {}, {}, {}
         grouped_w, w_codes, w_scales = {}, {}, {}
         acc, hidden, magnitude, root, shrink = {}, {}, {}, {}, {}
         grouped_h, h_codes, h_scales = {}, {}, {}
-        scores_ps = {}
+        scores = {}
+        ALL = slice(0, TOKENS)
+        Q = slice(0, SEQ)
+        K = slice(SEQ, TOKENS)
+        SETS = range(FEATURE_TILES)
 
-        def load_x(unit):
-            head, batch, side = place(unit)
-            source = (hq1, hk1)[side]
-            rows = inputs.tile([P, TOKEN_TILES, WIDTH], BF16, name="x_rows%d" % unit)
-            nc.sync.dma_start(out=rows[:], in_=source[batch, head].rearrange("(a p) k -> p a k", p=P))
-            x_rows[unit] = rows
+        def load_x(pair, side):
+            head, batch = pair // BATCH, pair % BATCH
+            rows = inputs.tile([P, TOKEN_TILES, WIDTH], BF16, name="x_rows%d_%d" % (pair, side))
+            source = (hq1, hk1)[side][batch, head]
+            nc.sync.dma_start(out=rows[:], in_=source.rearrange("(a p) k -> p a k", p=P))
+            x_rows[pair, side] = rows
 
         def load_w(head):
             rows = inputs.tile([P, PACK, WIDTH], BF16, name="w_rows%d" % head)
@@ -75,295 +71,315 @@ def tile_decoder_pb_kernel(tc, hq1, hk1, proj1, bias1, out):
                 nc.sync.dma_start(out=target, in_=source)
                 return
             for half in range(2):
-                cols = slice(half * PAIR * P, (half + 1) * PAIR * P)
+                cols = slice(half * HALF_WIDTH, (half + 1) * HALF_WIDTH)
                 for u in range(HALVES):
                     nc.sync.dma_start(out=target[:, u, :, cols], in_=source[:, u, :, cols])
 
-        load_x(0)
+        load_x(0, 0)
         load_w(0)
-        for unit in range(1, 4):
-            load_x(unit)
-        for head in range(1, HEADS):
-            load_w(head)
-            for unit in range(head * UNITS_PER_HEAD, (head + 1) * UNITS_PER_HEAD):
-                load_x(unit)
+        load_x(0, 1)
+        for head in range(HEADS):
+            if head > 0:
+                load_w(head)
+            for pair in range(max(1, head * BATCH), (head + 1) * BATCH):
+                for side in range(SIDES):
+                    load_x(pair, side)
 
         identity = consts.tile([P, P], F32)
         make_identity(nc, identity[:])
         bias_rows = consts.tile([P, PAIR * P], BF16)
         nc.vector.memset(bias_rows[:], 0.0)
-        one = consts.tile([P, 1], F32)
-        nc.vector.memset(one[:], 1.0 / GAMMA)
-
+        offset = consts.tile([P, 1], F32)
+        nc.vector.memset(offset[:], 1.0 / GAMMA)
         nc.scalar.dma_start(
             out=bias_rows[0 : HEADS * HALVES, :],
             in_=bias1.rearrange("o h i (u w) -> (o h i u) w", u=HALVES),
         )
         bias = consts.tile([P, HEADS * FEATURE_TILES], F32)
-
-        def turn_bias():
-            bias_t = psum_o.tile([P, P], F32, tag="product")
-            nc.tensor.transpose(out=bias_t[:], in_=bias_rows[:].bitcast(F32), identity=identity[:])
-            return bias_t
-        def copy_bias(bias_t):
-            nc.vector.tensor_copy(out=bias[:], in_=bias_t[:, 0 : HEADS * HALVES].bitcast(BF16))
-
         warm = consts.tile([P, 1], F32)
-        nc.scalar.activation(out=warm[:], in_=one[:], func=ACT.Abs_reciprocal_sqrt)
+        nc.scalar.activation(out=warm[:], in_=offset[:], func=ACT.Abs_reciprocal_sqrt)
 
-        def make_w(head):
-            w_codes[head] = pairs.tile([P, WIDTH], U32, align_bytes=64, name="w_codes")
-            w_scales[head] = pairs.tile([P, WIDTH], U8, align_bytes=64, name="w_scales")
+        def transpose_bias():
+            turned = psum_o.tile([P, P], F32, name="product")
+            nc.tensor.transpose(out=turned[:], in_=bias_rows[:].bitcast(F32), identity=identity[:])
+            return turned
 
-        def regroup_w(head, m, engine):
-            if head not in w_codes:
-                make_w(head)
-            grouped = (w_ring if engine == 'G' else wide).tile([P, P, PACK], BF16, align_bytes=64, name="grouped_w" + engine)
-            grouped_w[head, m] = grouped
+        def copy_bias(turned):
+            nc.vector.tensor_copy(out=bias[:], in_=turned[:, 0 : HEADS * HALVES].bitcast(BF16))
+
+        def regroup_w(head, engine, first, count):
+            if (head, first) not in grouped_w:
+                pool = ring if engine == "G" else deep2
+                grouped_w[head, first] = pool.tile([P, count * P, PACK], BF16, align_bytes=64, name="grouped_w%s%d" % (engine, count))
+            grouped = grouped_w[head, first]
             columns = w_rows[head][:].rearrange("p t (u q e) -> p t u q e", q=P, e=PAIR)
-            src = columns[:, :, m // PAIR, :, m % PAIR]
-            dst = grouped[:]
-            if engine == 'G':
-                nc.gpsimd.tensor_scalar(out=dst, in0=src.rearrange("p t q -> p q t"), scalar1=1.0, scalar2=0.0, op0=ALU.mult, op1=ALU.add)
-            else:
-                o = dst.rearrange("p (c i) t -> p c t i", i=RUN)
-                s = src.rearrange("p t (c i) -> p c t i", i=RUN)
-                if engine == 'V':
-                    nc.vector.tensor_copy(out=o, in_=s)
+            for m in range(first, first + count):
+                target = grouped[:, (m - first) * P : (m - first + 1) * P, :]
+                origin = columns[:, :, m // PAIR, :, m % PAIR]
+                if engine == "G":
+                    nc.gpsimd.tensor_scalar(out=target, in0=origin.rearrange("p t q -> p q t"), scalar1=1.0, scalar2=0.0, op0=ALU.mult, op1=ALU.add)
                 else:
-                    nc.scalar.copy(out=o, in_=s)
+                    o = target.rearrange("p (c i) t -> p c t i", i=COPY_RUN)
+                    s = origin.rearrange("p t (c i) -> p c t i", i=COPY_RUN)
+                    if engine == "V":
+                        nc.vector.tensor_copy(out=o, in_=s)
+                    else:
+                        nc.scalar.copy(out=o, in_=s)
 
-        def quantise_w(head, m):
-            cols = slice(m * P, (m + 1) * P)
+        def quantise_w(head, first, count):
+            if head not in w_codes:
+                w_codes[head] = deep2.tile([P, WIDTH], U32, align_bytes=64, name="w_codes")
+                w_scales[head] = deep2.tile([P, WIDTH], U8, align_bytes=64, name="w_scales")
+            cols = slice(first * P, (first + count) * P)
             nc.vector.quantize_mx(
                 out=w_codes[head][:, cols].bitcast(FP8X4),
                 scales=w_scales[head][:, cols],
-                in_=grouped_w[head, m][:].rearrange("p n t -> p (n t)"),
+                in_=grouped_w[head, first][:].rearrange("p n t -> p (n t)"),
             )
 
-        def transpose_x(unit):
-            if not live(unit):
+        def transpose_x(pair, side):
+            if pair >= PAIRS:
                 return
             turned = psum_t.tile([P, TOKEN_TILES, HALVES, P], F32, name="turned")
             for a in range(TOKEN_TILES):
-                words = x_rows[unit][:, a, :].bitcast(F32)
+                words = x_rows[pair, side][:, a, :].bitcast(F32)
                 for u in range(HALVES):
                     nc.tensor.transpose(out=turned[:, a, u, :], in_=words[:, u * P : (u + 1) * P], identity=identity[:])
-            x_t[unit] = turned
+            turned_x[pair, side] = turned
 
-        def regroup_x(unit, want):
-            if not live(unit):
+        def regroup_x(pair, side, engine):
+            if pair >= PAIRS:
                 return
-            if want != ('S' if unit % 2 == 0 else 'V'):
-                return
-            grouped = quads.tile([P, SEQ, PACK], BF16, align_bytes=64, name="grouped_x")
-            target = grouped[:].rearrange("p s t -> p (s t)").bitcast(F32).rearrange("p (a r u) -> p a r u", a=TOKEN_TILES, u=HALVES)
-            origin = x_t[unit][:].rearrange("p a u r -> p a r u")
-            if want == 'S':
+            if pair not in grouped_x:
+                grouped_x[pair] = deep3.tile([P, TOKENS, PACK], BF16, align_bytes=64, name="grouped_x")
+            words = grouped_x[pair][:].rearrange("p s t -> p (s t)").bitcast(F32)
+            n = SEQ * HALVES
+            target = words[:, side * n : (side + 1) * n].rearrange("p (a r u) -> p a r u", a=TOKEN_TILES, u=HALVES)
+            origin = turned_x[pair, side][:].rearrange("p a u r -> p a r u")
+            if engine == "S":
                 nc.scalar.copy(out=target, in_=origin)
             else:
                 nc.vector.tensor_copy(out=target, in_=origin)
-            grouped_x[unit] = grouped
 
-        def quantise_x(unit):
-            if not live(unit):
+        def quantise_x(pair, tok):
+            if pair >= PAIRS:
                 return
-            codes = pairs.tile([P, SEQ], U32, align_bytes=64, name="x_codes")
-            scales = pairs.tile([P, SEQ], U8, align_bytes=64, name="x_scales")
-            nc.vector.quantize_mx(out=codes[:].bitcast(FP8X4), scales=scales[:], in_=grouped_x[unit][:].rearrange("p s t -> p (s t)"))
-            x_codes[unit], x_scales[unit] = codes, scales
+            if pair not in x_codes:
+                x_codes[pair] = deep2.tile([P, TOKENS], U32, align_bytes=64, name="x_codes")
+                x_scales[pair] = deep2.tile([P, TOKENS], U8, align_bytes=64, name="x_scales")
+            nc.vector.quantize_mx(
+                out=x_codes[pair][:, tok].bitcast(FP8X4),
+                scales=x_scales[pair][:, tok],
+                in_=grouped_x[pair][:, tok, :].rearrange("p s t -> p (s t)"),
+            )
 
-        def project(unit, ms=(0, 1, 2, 3)):
-            if not live(unit):
+        def project(pair, ms, tok):
+            if pair >= PAIRS:
                 return
-            head = place(unit)[0]
-            acc.setdefault(unit, {})
+            head = pair // BATCH
             for m in ms:
-                if m % 2 == 0:
-                    acc[unit]['b'] = psum_h.tile([P, 2, SEQ], F32, name="sums")
-                sums = acc[unit]['b']
+                if (pair, m) not in acc:
+                    acc[pair, m] = psum_h.tile([P, TOKENS], F32, name="sums")
                 cols = slice(m * P, (m + 1) * P)
                 nc.tensor.matmul_mx(
-                    out=sums[:, m % 2, :],
+                    out=acc[pair, m][:, tok],
                     lhsT=w_codes[head][:, cols].bitcast(FP8X4),
                     lhsT_scale=w_scales[head][:, cols],
-                    rhs=x_codes[unit][:].bitcast(FP8X4),
-                    rhs_scale=x_scales[unit][:],
+                    rhs=x_codes[pair][:, tok].bitcast(FP8X4),
+                    rhs_scale=x_scales[pair][:, tok],
                     start=True,
                     stop=True,
                 )
-                acc[unit][m] = sums[:, m % 2, :]
 
-        def add(unit, ms=(0, 1, 2, 3), tok=slice(0, SEQ)):
-            if not live(unit):
+        def add(pair, ms, tok):
+            if pair >= PAIRS:
                 return
-            head = place(unit)[0]
-            if unit not in hidden:
-                hidden[unit] = quads.tile([P, FEATURE_TILES, SEQ], F32, name="hidden")
-                magnitude[unit] = pairs.tile([P, FEATURE_TILES, SEQ], F32, name="magnitude")
-                root[unit] = pairs.tile([P, FEATURE_TILES, SEQ], F32, name="root")
-                shrink[unit] = pairs.tile([P, FEATURE_TILES, SEQ], F32, name="shrink")
+            if pair not in hidden:
+                hidden[pair] = deep3.tile([P, FEATURE_TILES, TOKENS], F32, name="hidden")
+                magnitude[pair] = deep2.tile([P, FEATURE_TILES, TOKENS], F32, name="magnitude")
+                root[pair] = deep2.tile([P, FEATURE_TILES, TOKENS], F32, name="root")
+                shrink[pair] = deep2.tile([P, FEATURE_TILES, TOKENS], F32, name="shrink")
             for m in ms:
-                column = head * FEATURE_TILES + m
+                column = pair // BATCH * FEATURE_TILES + m
                 nc.vector.scalar_tensor_tensor(
-                    out=hidden[unit][:, m, tok],
-                    in0=acc[unit][m][:, tok],
+                    out=hidden[pair][:, m, tok],
+                    in0=acc[pair, m][:, tok],
                     scalar=bias[:, column : column + 1],
-                    in1=grouped_x[unit][:, tok, m],
+                    in1=grouped_x[pair][:, tok, m],
                     op0=ALU.add,
                     op1=ALU.add,
                 )
 
-        def take_magnitude(unit, tok=slice(0, SEQ), ms=slice(0, 4)):
-            if not live(unit):
-                return
-            nc.scalar.activation(out=magnitude[unit][:, ms, tok], in_=hidden[unit][:, ms, tok], func=ACT.Abs)
+        def magnify(pair, ms, tok, engine="S"):
+            h, a = hidden[pair][:, ms, tok], magnitude[pair][:, ms, tok]
+            if engine == "S":
+                nc.scalar.activation(out=a, in_=h, func=ACT.Abs)
+            else:
+                nc.vector.scalar_tensor_tensor(out=a, in0=h, scalar=-1.0, in1=h, op0=ALU.mult, op1=ALU.max)
 
-        def take_root(unit, tok=slice(0, SEQ), ms=slice(0, 4)):
-            if not live(unit):
-                return
-            nc.scalar.activation(out=root[unit][:, ms, tok], in_=magnitude[unit][:, ms, tok], func=ACT.Abs_reciprocal_sqrt, bias=one[:, 0:1])
+        def take_root(pair, ms, tok):
+            nc.scalar.activation(
+                out=root[pair][:, ms, tok],
+                in_=magnitude[pair][:, ms, tok],
+                func=ACT.Abs_reciprocal_sqrt,
+                bias=offset[:, 0:1],
+            )
 
-        def take_shrink(unit, tok=slice(0, SEQ), ms=slice(0, 4)):
-            if not live(unit):
-                return
-            nc.scalar.activation(out=shrink[unit][:, ms, tok], in_=root[unit][:, ms, tok], func=ACT.Square)
+        def take_shrink(pair, ms, tok, engine="S"):
+            r, s = root[pair][:, ms, tok], shrink[pair][:, ms, tok]
+            if engine == "S":
+                nc.scalar.activation(out=s, in_=r, func=ACT.Square)
+            else:
+                nc.gpsimd.tensor_tensor(out=s, in0=r, in1=r, op=ALU.mult)
 
-        def squash(unit, tok=slice(0, SEQ)):
-            if not live(unit):
+        def squash(pair, tok):
+            if pair < 0:
                 return
-            if unit not in grouped_h:
-                side = place(unit)[2]
-                grouped_h[unit] = pairs.tile([P, SEQ, PACK], BF16, align_bytes=64, name="grouped_h")
-                h_codes[unit] = pairs.tile([P, SEQ], U32, align_bytes=64, name="h_codes%d" % side)
-                h_scales[unit] = pairs.tile([P, SEQ], U8, align_bytes=64, name="h_scales%d" % side)
+            if pair not in grouped_h:
+                grouped_h[pair] = deep2.tile([P, TOKENS, PACK], BF16, align_bytes=64, name="grouped_h")
+                h_codes[pair] = deep2.tile([P, TOKENS], U32, align_bytes=64, name="h_codes")
+                h_scales[pair] = deep2.tile([P, TOKENS], U8, align_bytes=64, name="h_scales")
             nc.vector.tensor_tensor(
-                out=grouped_h[unit][:, tok, :].rearrange("p (c i) t -> p c t i", i=RUN),
-                in0=hidden[unit][:, :, tok].rearrange("p t (c i) -> p c t i", i=RUN),
-                in1=shrink[unit][:, :, tok].rearrange("p t (c i) -> p c t i", i=RUN),
+                out=grouped_h[pair][:, tok, :].rearrange("p (c i) t -> p c t i", i=WORD_RUN),
+                in0=hidden[pair][:, :, tok].rearrange("p t (c i) -> p c t i", i=WORD_RUN),
+                in1=shrink[pair][:, :, tok].rearrange("p t (c i) -> p c t i", i=WORD_RUN),
                 op=ALU.mult,
             )
 
-        def quantise_h(unit, tok=slice(0, SEQ)):
-            if not live(unit):
+        def quantise_h(pair, tok):
+            if pair < 0:
                 return
             nc.vector.quantize_mx(
-                out=h_codes[unit][:, tok].bitcast(FP8X4),
-                scales=h_scales[unit][:, tok],
-                in_=grouped_h[unit][:, tok, :].rearrange("p s t -> p (s t)"),
+                out=h_codes[pair][:, tok].bitcast(FP8X4),
+                scales=h_scales[pair][:, tok],
+                in_=grouped_h[pair][:, tok, :].rearrange("p s t -> p (s t)"),
             )
 
-        def score(key_unit, tok=slice(0, SEQ)):
-            if not live(key_unit) or place(key_unit)[2] == 0:
+        def score(pair, keys):
+            if pair < 0:
                 return
-            query_unit = key_unit - 1
-            if tok.stop - tok.start == SEQ:
-                product = psum_o.tile([P, TOKEN_TILES, SEQ], F32, name="product")
-            else:
-                product = psum_o.tile([P, TOKEN_TILES, HALF], F32, name="product")
+            n = keys.stop - keys.start
+            product = psum_o.tile([P, TOKEN_TILES, n], F32, name="product")
             for a in range(TOKEN_TILES):
                 cols = slice(a * P, (a + 1) * P)
                 nc.tensor.matmul_mx(
                     out=product[:, a, :],
-                    lhsT=h_codes[query_unit][:, cols].bitcast(FP8X4),
-                    lhsT_scale=h_scales[query_unit][:, cols],
-                    rhs=h_codes[key_unit][:, tok].bitcast(FP8X4),
-                    rhs_scale=h_scales[key_unit][:, tok],
+                    lhsT=h_codes[pair][:, cols].bitcast(FP8X4),
+                    lhsT_scale=h_scales[pair][:, cols],
+                    rhs=h_codes[pair][:, keys].bitcast(FP8X4),
+                    rhs_scale=h_scales[pair][:, keys],
                     start=True,
                     stop=True,
                 )
-            scores_ps[key_unit, tok.start] = product
+            scores[pair, keys.start] = product
 
-        def store(key_unit, want, tok=slice(0, SEQ)):
-            if not live(key_unit) or place(key_unit)[2] == 0:
+        def store(pair, keys, engine):
+            if pair < 0:
                 return
-            if want != 'V':
-                return
-            head, batch = place(key_unit)[0:2]
-            result = pairs.tile([P, TOKEN_TILES, SEQ], F32, name="result")
-            n = tok.stop - tok.start
-            nc.vector.tensor_copy(out=result[:, :, 0:n], in_=scores_ps[key_unit, tok.start][:])
-            nc.sync.dma_start(out=out[batch, head].rearrange("(a p) t -> p a t", p=P)[:, :, tok], in_=result[:, :, 0:n])
+            head, batch = pair // BATCH, pair % BATCH
+            n = keys.stop - keys.start
+            result = deep2.tile([P, TOKEN_TILES, n], F32, name="result%d" % n)
+            if engine == "S":
+                nc.scalar.copy(out=result[:], in_=scores[pair, keys.start][:])
+            else:
+                nc.vector.tensor_copy(out=result[:], in_=scores[pair, keys.start][:])
+            nc.sync.dma_start(
+                out=out[batch, head].rearrange("(a p) t -> p a t", p=P)[:, :, keys.start - SEQ : keys.stop - SEQ],
+                in_=result[:],
+            )
 
-        W0S = (2,)
-        transpose_x(0)
-        bias_t = turn_bias()
-        regroup_x(0, 'S')
-        regroup_w(0, 0, 'V')
-        regroup_w(0, 1, 'V')
-        for m in W0S:
-            regroup_w(0, m, 'S')
-        quantise_x(0)
-        quantise_w(0, 0)
-        quantise_w(0, 1)
-        project(0, (0, 1))
-        transpose_x(1)
+        LO, HI, EVERY = slice(0, 2), slice(2, 4), slice(0, 4)
+        transpose_x(0, 0)
+        bias_t = transpose_bias()
+        regroup_x(0, 0, "S")
+        regroup_w(0, "V", 0, 2)
+        regroup_w(0, "S", 2, 1)
+        quantise_x(0, Q)
+        quantise_w(0, 0, 2)
+        transpose_x(0, 1)
+        project(0, (0, 1), Q)
         copy_bias(bias_t)
-        for m in (2, 3):
-            if m not in W0S:
-                regroup_w(0, m, 'V')
-        add(0, (0, 1))
-        take_magnitude(0, ms=slice(0, 2))
-        quantise_w(0, 2)
-        quantise_w(0, 3)
-        project(0, (2, 3))
-        transpose_x(2)
-        regroup_x(1, 'V')
-        regroup_x(1, 'S')
-        add(0, (2, 3))
-        take_magnitude(0, ms=slice(2, 4))
-        quantise_x(1)
-        project(1)
-        regroup_x(2, 'S')
-        regroup_x(2, 'V')
-        for i in range(0, UNITS + 3):
-            if i < UNITS - 1:
-                transpose_x(i + 3)
-                squash(i - 2)
-                if i > 0:
-                    take_magnitude(i)
-                if 2 < i < 11:
-                    quantise_w((i + 5) // 4, (i + 1) % 4)
-                if 1 < i < 10:
-                    regroup_w((i + 6) // 4, (i + 2) % 4, 'G')
-                add(i + 1)
-                take_shrink(i - 1)
-                if 0 <= i < 2:
-                    regroup_w(1, 2 * i, 'V')
-                    regroup_w(1, 2 * i + 1, 'V')
-                quantise_h(i - 2)
-                score(i - 2)
-                take_root(i)
-                if 1 <= i < 3:
-                    quantise_w(1, 2 * i - 2)
-                    quantise_w(1, 2 * i - 1)
-                quantise_x(i + 2)
-                project(i + 2)
-                regroup_x(i + 3, 'S')
-                regroup_x(i + 3, 'V')
-                store(i - 3, 'V')
-                store(i - 3, 'S')
-            elif i == UNITS - 1:
-                a, b = slice(0, HALF), slice(HALF, SEQ)
-                squash(i - 2)
-                take_magnitude(i, a)
-                take_shrink(i - 1)
-                take_root(i, a)
-                take_magnitude(i, b)
-                quantise_h(i - 2)
-                score(i - 2)
-                store(i - 3, 'V')
-                store(i - 3, 'S')
-                take_shrink(i, a)
-                squash(i - 1)
-                take_root(i, b)
-                quantise_h(i - 1)
-                store(i - 2, 'V')
-                store(i - 2, 'S')
-                take_shrink(i, b)
-                for t in (a, b):
-                    squash(i, t)
-                    quantise_h(i, t)
-                    score(i, t)
-                    store(i, 'V', t)
-                    store(i, 'S', t)
+        regroup_x(0, 1, "S")
+        add(0, (0, 1), Q)
+        regroup_w(0, "V", 3, 1)
+        magnify(0, LO, Q)
+        quantise_w(0, 2, 1)
+        quantise_x(0, K)
+        quantise_w(0, 3, 1)
+        project(0, (2, 3), Q)
+        project(0, SETS, K)
+        transpose_x(1, 0)
+        transpose_x(1, 1)
+        add(0, (2, 3), Q)
+        magnify(0, HI, Q)
+        take_root(0, EVERY, Q)
+        add(0, SETS, K)
+        take_shrink(0, EVERY, Q)
+        magnify(0, EVERY, K)
+        regroup_x(1, 0, "V")
+        regroup_x(1, 1, "V")
+        quantise_x(1, ALL)
+        project(1, SETS, ALL)
+        take_root(0, EVERY, K)
+        take_shrink(0, EVERY, K)
+        transpose_x(2, 0)
+        transpose_x(2, 1)
+        regroup_w(1, "V", 0, 2)
+        add(1, SETS, ALL)
+        regroup_x(2, 0, "S")
+        regroup_x(2, 1, "V")
+        regroup_w(1, "V", 2, 2)
+        quantise_w(1, 0, 2)
+        quantise_x(2, ALL)
+        quantise_w(1, 2, 2)
+        project(2, SETS, ALL)
+        regroup_w(2, "G", 0, 2)
+        for j in range(1, PAIRS - 1):
+            transpose_x(j + 2, 0)
+            transpose_x(j + 2, 1)
+            squash(j - 1, ALL)
+            if j in (1, 2, 3, 4):
+                quantise_w(j // 2 + 1 if j % 2 == 0 else (j + 3) // 2, 0 if j % 2 else 2, 2)
+            if j in (1, 2, 3):
+                regroup_w((j + 4) // 2, "G", 2 if j % 2 else 0, 2)
+            magnify(j, LO, ALL)
+            magnify(j, HI, ALL)
+            take_root(j, LO, ALL)
+            add(j + 1, SETS, ALL)
+            quantise_h(j - 1, ALL)
+            score(j - 1, K)
+            take_root(j, HI, ALL)
+            take_shrink(j, LO, ALL)
+            regroup_x(j + 2, 0, "S")
+            take_shrink(j, HI, ALL)
+            regroup_x(j + 2, 1, "V")
+            if j > 1:
+                store(j - 2, K, "V")
+            quantise_x(j + 2, ALL)
+            project(j + 2, SETS, ALL)
+        j = PAIRS - 1
+        KA, KB = slice(SEQ, SEQ + P), slice(SEQ + P, TOKENS)
+        squash(j - 1, ALL)
+        magnify(j, EVERY, Q)
+        magnify(j, EVERY, KA)
+        take_root(j, EVERY, Q)
+        store(j - 2, K, "V")
+        quantise_h(j - 1, ALL)
+        score(j - 1, K)
+        magnify(j, EVERY, KB)
+        take_shrink(j, EVERY, Q)
+        take_root(j, EVERY, KA)
+        take_root(j, EVERY, KB)
+        squash(j, Q)
+        store(j - 1, K, "V")
+        quantise_h(j, Q)
+        take_shrink(j, EVERY, KA)
+        take_shrink(j, EVERY, KB)
+        squash(j, KA)
+        quantise_h(j, KA)
+        score(j, KA)
+        squash(j, KB)
+        store(j, KA, "V")
+        quantise_h(j, KB)
+        score(j, KB)
+        store(j, KB, "V")

@@ -40,6 +40,7 @@ def tile_decoder_pb_kernel(tc, hq1, hk1, proj1, bias1, out):
         ring = ctx.enter_context(tc.tile_pool(name="ring", bufs=1))
         deep2 = ctx.enter_context(tc.tile_pool(name="deep2", bufs=2))
         deep3 = ctx.enter_context(tc.tile_pool(name="deep3", bufs=3))
+        deep4 = ctx.enter_context(tc.tile_pool(name="deep4", bufs=4))
         psum_t = ctx.enter_context(tc.psum_pool(name="psum_t", bufs=2))
         psum_h = ctx.enter_context(tc.psum_pool(name="psum_h", bufs=4))
         psum_o = ctx.enter_context(tc.psum_pool(name="psum_o", bufs=2))
@@ -49,7 +50,7 @@ def tile_decoder_pb_kernel(tc, hq1, hk1, proj1, bias1, out):
         grouped_w, w_codes, w_scales = {}, {}, {}
         acc, hidden, magnitude, root, shrink = {}, {}, {}, {}, {}
         grouped_h, h_codes, h_scales = {}, {}, {}
-        scores = {}
+        scores, gshrink = {}, {}
         ALL = slice(0, TOKENS)
         Q = slice(0, SEQ)
         K = slice(SEQ, TOKENS)
@@ -151,7 +152,7 @@ def tile_decoder_pb_kernel(tc, hq1, hk1, proj1, bias1, out):
             if pair >= PAIRS:
                 return
             if pair not in grouped_x:
-                grouped_x[pair] = deep3.tile([P, TOKENS, PACK], BF16, align_bytes=64, name="grouped_x")
+                grouped_x[pair] = deep4.tile([P, TOKENS, PACK], BF16, align_bytes=64, name="grouped_x")
             words = grouped_x[pair][:].rearrange("p s t -> p (s t)").bitcast(F32)
             n = SEQ * HALVES
             target = words[:, side * n : (side + 1) * n].rearrange("p (a r u) -> p a r u", a=TOKEN_TILES, u=HALVES)
@@ -199,6 +200,7 @@ def tile_decoder_pb_kernel(tc, hq1, hk1, proj1, bias1, out):
                 magnitude[pair] = deep2.tile([P, FEATURE_TILES, TOKENS], F32, name="magnitude")
                 root[pair] = deep2.tile([P, FEATURE_TILES, TOKENS], F32, name="root")
                 shrink[pair] = deep2.tile([P, FEATURE_TILES, TOKENS], F32, name="shrink")
+                gshrink[pair] = ring.tile([P, FEATURE_TILES, SEQ], F32, name="gshrink")
             for m in ms:
                 column = pair // BATCH * FEATURE_TILES + m
                 nc.vector.scalar_tensor_tensor(
@@ -227,12 +229,14 @@ def tile_decoder_pb_kernel(tc, hq1, hk1, proj1, bias1, out):
 
         def take_shrink(pair, ms, tok, engine="S"):
             r, s = root[pair][:, ms, tok], shrink[pair][:, ms, tok]
+            if engine == "G":
+                s = gshrink[pair][:, ms, 0 : tok.stop - tok.start]
             if engine == "S":
                 nc.scalar.activation(out=s, in_=r, func=ACT.Square)
             else:
                 nc.gpsimd.tensor_tensor(out=s, in0=r, in1=r, op=ALU.mult)
 
-        def squash(pair, tok):
+        def squash(pair, tok, engine="S"):
             if pair < 0:
                 return
             if pair not in grouped_h:
@@ -242,7 +246,7 @@ def tile_decoder_pb_kernel(tc, hq1, hk1, proj1, bias1, out):
             nc.vector.tensor_tensor(
                 out=grouped_h[pair][:, tok, :].rearrange("p (c i) t -> p c t i", i=WORD_RUN),
                 in0=hidden[pair][:, :, tok].rearrange("p t (c i) -> p c t i", i=WORD_RUN),
-                in1=shrink[pair][:, :, tok].rearrange("p t (c i) -> p c t i", i=WORD_RUN),
+                in1=(shrink[pair][:, :, tok] if engine == "S" else gshrink[pair][:, :, 0 : tok.stop - tok.start]).rearrange("p t (c i) -> p c t i", i=WORD_RUN),
                 op=ALU.mult,
             )
 
@@ -288,98 +292,120 @@ def tile_decoder_pb_kernel(tc, hq1, hk1, proj1, bias1, out):
                 in_=result[:],
             )
 
+        GS = [0] * PAIRS
+        XE = ["SV"] * 4 + ["VV"] * 4
+        X2 = "SV"
+        SE = "V"
+        VT = "V"
+
         LO, HI, EVERY = slice(0, 2), slice(2, 4), slice(0, 4)
         transpose_x(0, 0)
         bias_t = transpose_bias()
         regroup_x(0, 0, "S")
         regroup_w(0, "V", 0, 2)
+        copy_bias(bias_t)
         regroup_w(0, "S", 2, 1)
         quantise_x(0, Q)
         quantise_w(0, 0, 2)
         transpose_x(0, 1)
         project(0, (0, 1), Q)
-        copy_bias(bias_t)
         regroup_x(0, 1, "S")
-        add(0, (0, 1), Q)
         regroup_w(0, "V", 3, 1)
-        magnify(0, LO, Q)
         quantise_w(0, 2, 1)
-        quantise_x(0, K)
         quantise_w(0, 3, 1)
         project(0, (2, 3), Q)
-        project(0, SETS, K)
         transpose_x(1, 0)
-        transpose_x(1, 1)
-        add(0, (2, 3), Q)
+        add(0, SETS, Q)
+        magnify(0, LO, Q)
         magnify(0, HI, Q)
-        take_root(0, EVERY, Q)
-        add(0, SETS, K)
-        take_shrink(0, EVERY, Q)
-        magnify(0, EVERY, K)
+        quantise_x(0, K)
+        transpose_x(1, 1)
+        project(0, SETS, K)
         regroup_x(1, 0, "V")
         regroup_x(1, 1, "V")
-        quantise_x(1, ALL)
-        project(1, SETS, ALL)
-        take_root(0, EVERY, K)
-        take_shrink(0, EVERY, K)
         transpose_x(2, 0)
         transpose_x(2, 1)
-        regroup_w(1, "V", 0, 2)
+        add(0, (0,), K)
+        quantise_x(1, ALL)
+        add(0, (1, 2, 3), K)
+        project(1, SETS, ALL)
+        take_root(0, EVERY, Q)
+        regroup_x(2, 0, X2[0])
+        take_shrink(0, EVERY, Q)
+        magnify(0, EVERY, K)
+        regroup_x(2, 1, X2[1])
+        take_root(0, EVERY, K)
         add(1, SETS, ALL)
-        regroup_x(2, 0, "S")
-        regroup_x(2, 1, "V")
+        magnify(1, EVERY, K)
+        take_shrink(0, EVERY, K)
+        regroup_w(1, "V", 0, 2)
         regroup_w(1, "V", 2, 2)
         quantise_w(1, 0, 2)
         quantise_x(2, ALL)
         quantise_w(1, 2, 2)
+        transpose_x(3, 0)
+        transpose_x(3, 1)
         project(2, SETS, ALL)
         regroup_w(2, "G", 0, 2)
+
+
+        def gsplit(j):
+            return slice(0, TOKENS - GS[j]), slice(TOKENS - GS[j], TOKENS)
+        def squashes(j):
+            s, g = gsplit(j)
+            squash(j, s)
+            if GS[j]:
+                squash(j, g, "G")
         for j in range(1, PAIRS - 1):
-            transpose_x(j + 2, 0)
-            transpose_x(j + 2, 1)
-            squash(j - 1, ALL)
+            s, g = gsplit(j)
+            squashes(j - 1)
             if j in (1, 2, 3, 4):
                 quantise_w(j // 2 + 1 if j % 2 == 0 else (j + 3) // 2, 0 if j % 2 else 2, 2)
+            if j > 1:
+                magnify(j, EVERY, K)
+            magnify(j, EVERY, Q)
+            take_root(j, EVERY, K)
+            if GS[j]:
+                take_shrink(j, EVERY, g, "G")
             if j in (1, 2, 3):
                 regroup_w((j + 4) // 2, "G", 2 if j % 2 else 0, 2)
-            magnify(j, LO, ALL)
-            magnify(j, HI, ALL)
-            take_root(j, LO, ALL)
+            take_root(j, EVERY, Q)
             add(j + 1, SETS, ALL)
+            if j > 1:
+                store(j - 2, K, SE)
+            regroup_x(j + 2, 0, XE[j][0])
+            regroup_x(j + 2, 1, XE[j][1])
+            take_shrink(j, EVERY, s)
             quantise_h(j - 1, ALL)
             score(j - 1, K)
-            take_root(j, HI, ALL)
-            take_shrink(j, LO, ALL)
-            regroup_x(j + 2, 0, "S")
-            take_shrink(j, HI, ALL)
-            regroup_x(j + 2, 1, "V")
-            if j > 1:
-                store(j - 2, K, "V")
             quantise_x(j + 2, ALL)
+            transpose_x(j + 3, 0)
+            transpose_x(j + 3, 1)
             project(j + 2, SETS, ALL)
+
         j = PAIRS - 1
         KA, KB = slice(SEQ, SEQ + P), slice(SEQ + P, TOKENS)
-        squash(j - 1, ALL)
+        squashes(j - 1)
         magnify(j, EVERY, Q)
         magnify(j, EVERY, KA)
         take_root(j, EVERY, Q)
         store(j - 2, K, "V")
         quantise_h(j - 1, ALL)
         score(j - 1, K)
-        magnify(j, EVERY, KB)
+        magnify(j, EVERY, KB, VT)
         take_shrink(j, EVERY, Q)
         take_root(j, EVERY, KA)
         take_root(j, EVERY, KB)
+        take_shrink(j, EVERY, KA)
         squash(j, Q)
         store(j - 1, K, "V")
         quantise_h(j, Q)
-        take_shrink(j, EVERY, KA)
         take_shrink(j, EVERY, KB)
         squash(j, KA)
+        squash(j, KB)
         quantise_h(j, KA)
         score(j, KA)
-        squash(j, KB)
-        store(j, KA, "V")
         quantise_h(j, KB)
         score(j, KB)
+        store(j, KA, "V")
         store(j, KB, "V")

@@ -27,7 +27,7 @@ TOKENS = SIDES * SEQ
 PAIRS = HEADS * BATCH
 HALF_WIDTH = WIDTH // HALVES
 COPY_RUN = 4
-WORD_RUN = 4
+WORD_RUN = 2
 
 FLOPS = 2 * PAIRS * TOKENS * WIDTH * WIDTH + 2 * PAIRS * SEQ * SEQ * WIDTH
 
@@ -50,7 +50,7 @@ def tile_decoder_pb_kernel(tc, hq1, hk1, proj1, bias1, out):
         grouped_w, w_codes, w_scales = {}, {}, {}
         acc, hidden, magnitude, root, shrink = {}, {}, {}, {}, {}
         grouped_h, h_codes, h_scales = {}, {}, {}
-        scores, gshrink = {}, {}
+        scores = {}
         ALL = slice(0, TOKENS)
         Q = slice(0, SEQ)
         K = slice(SEQ, TOKENS)
@@ -200,7 +200,6 @@ def tile_decoder_pb_kernel(tc, hq1, hk1, proj1, bias1, out):
                 magnitude[pair] = deep2.tile([P, FEATURE_TILES, TOKENS], F32, name="magnitude")
                 root[pair] = deep2.tile([P, FEATURE_TILES, TOKENS], F32, name="root")
                 shrink[pair] = deep2.tile([P, FEATURE_TILES, TOKENS], F32, name="shrink")
-                gshrink[pair] = ring.tile([P, FEATURE_TILES, SEQ], F32, name="gshrink")
             for m in ms:
                 column = pair // BATCH * FEATURE_TILES + m
                 nc.vector.scalar_tensor_tensor(
@@ -229,14 +228,12 @@ def tile_decoder_pb_kernel(tc, hq1, hk1, proj1, bias1, out):
 
         def take_shrink(pair, ms, tok, engine="S"):
             r, s = root[pair][:, ms, tok], shrink[pair][:, ms, tok]
-            if engine == "G":
-                s = gshrink[pair][:, ms, 0 : tok.stop - tok.start]
             if engine == "S":
                 nc.scalar.activation(out=s, in_=r, func=ACT.Square)
             else:
                 nc.gpsimd.tensor_tensor(out=s, in0=r, in1=r, op=ALU.mult)
 
-        def squash(pair, tok, engine="S"):
+        def squash(pair, tok):
             if pair < 0:
                 return
             if pair not in grouped_h:
@@ -246,7 +243,7 @@ def tile_decoder_pb_kernel(tc, hq1, hk1, proj1, bias1, out):
             nc.vector.tensor_tensor(
                 out=grouped_h[pair][:, tok, :].rearrange("p (c i) t -> p c t i", i=WORD_RUN),
                 in0=hidden[pair][:, :, tok].rearrange("p t (c i) -> p c t i", i=WORD_RUN),
-                in1=(shrink[pair][:, :, tok] if engine == "S" else gshrink[pair][:, :, 0 : tok.stop - tok.start]).rearrange("p t (c i) -> p c t i", i=WORD_RUN),
+                in1=shrink[pair][:, :, tok].rearrange("p t (c i) -> p c t i", i=WORD_RUN),
                 op=ALU.mult,
             )
 
@@ -292,11 +289,12 @@ def tile_decoder_pb_kernel(tc, hq1, hk1, proj1, bias1, out):
                 in_=result[:],
             )
 
-        GS = [0] * PAIRS
-        XE = ["SV"] * 4 + ["VV"] * 4
+        GS = [0] * 4 + [SEQ] * 3 + [0]
+        XE = ["SV"] * PAIRS
         X2 = "SV"
         SE = "V"
-        VT = "V"
+        VT = "S"
+
 
         LO, HI, EVERY = slice(0, 2), slice(2, 4), slice(0, 4)
         transpose_x(0, 0)
@@ -348,17 +346,11 @@ def tile_decoder_pb_kernel(tc, hq1, hk1, proj1, bias1, out):
         project(2, SETS, ALL)
         regroup_w(2, "G", 0, 2)
 
-
         def gsplit(j):
             return slice(0, TOKENS - GS[j]), slice(TOKENS - GS[j], TOKENS)
-        def squashes(j):
-            s, g = gsplit(j)
-            squash(j, s)
-            if GS[j]:
-                squash(j, g, "G")
         for j in range(1, PAIRS - 1):
             s, g = gsplit(j)
-            squashes(j - 1)
+            squash(j - 1, ALL)
             if j in (1, 2, 3, 4):
                 quantise_w(j // 2 + 1 if j % 2 == 0 else (j + 3) // 2, 0 if j % 2 else 2, 2)
             if j > 1:
@@ -385,7 +377,7 @@ def tile_decoder_pb_kernel(tc, hq1, hk1, proj1, bias1, out):
 
         j = PAIRS - 1
         KA, KB = slice(SEQ, SEQ + P), slice(SEQ + P, TOKENS)
-        squashes(j - 1)
+        squash(j - 1, ALL)
         magnify(j, EVERY, Q)
         magnify(j, EVERY, KA)
         take_root(j, EVERY, Q)

@@ -63,25 +63,25 @@ def tile_decoder_pb_kernel(tc, hq1, hk1, proj1, bias1, out):
             nc.sync.dma_start(out=rows[:], in_=source.rearrange("(a p) k -> p a k", p=P))
             x_rows[pair, side] = rows
 
-        def load_w(head):
-            rows = inputs.tile([P, PACK, WIDTH], BF16, name="w_rows%d" % head)
-            w_rows[head] = rows
+        def load_w(head, halves):
+            if head not in w_rows:
+                w_rows[head] = inputs.tile([P, PACK, WIDTH], BF16, name="w_rows%d" % head)
             source = proj1[0, head].rearrange("(u p e) n -> p u e n", p=P, e=PAIR)
-            target = rows[:].rearrange("p (u e) n -> p u e n", e=PAIR)
-            if head > 0:
+            target = w_rows[head][:].rearrange("p (u e) n -> p u e n", e=PAIR)
+            if len(halves) == 2:
                 nc.sync.dma_start(out=target, in_=source)
                 return
-            for half in range(2):
-                cols = slice(half * HALF_WIDTH, (half + 1) * HALF_WIDTH)
-                for u in range(HALVES):
-                    nc.sync.dma_start(out=target[:, u, :, cols], in_=source[:, u, :, cols])
+            cols = slice(halves[0] * HALF_WIDTH, (halves[0] + 1) * HALF_WIDTH)
+            for u in range(HALVES):
+                nc.sync.dma_start(out=target[:, u, :, cols], in_=source[:, u, :, cols])
 
         load_x(0, 0)
-        load_w(0)
+        load_w(0, (0,))
+        load_w(0, (1,))
         load_x(0, 1)
         for head in range(HEADS):
             if head > 0:
-                load_w(head)
+                load_w(head, (0, 1))
             for pair in range(max(1, head * BATCH), (head + 1) * BATCH):
                 for side in range(SIDES):
                     load_x(pair, side)
@@ -289,8 +289,8 @@ def tile_decoder_pb_kernel(tc, hq1, hk1, proj1, bias1, out):
                 in_=result[:],
             )
 
-        GS = [0] * 4 + [SEQ] * 3 + [0]
-        XE = ["SV"] * PAIRS
+        GS = [0] + [P] * 3 + [SEQ] * 3 + [0]
+        XE = ["SV"] * 4 + ["SS"] * 4
         X2 = "SV"
         SE = "V"
         VT = "S"
@@ -350,17 +350,17 @@ def tile_decoder_pb_kernel(tc, hq1, hk1, proj1, bias1, out):
             return slice(0, TOKENS - GS[j]), slice(TOKENS - GS[j], TOKENS)
         for j in range(1, PAIRS - 1):
             s, g = gsplit(j)
-            squash(j - 1, ALL)
             if j in (1, 2, 3, 4):
                 quantise_w(j // 2 + 1 if j % 2 == 0 else (j + 3) // 2, 0 if j % 2 else 2, 2)
+            squash(j - 1, ALL)
             if j > 1:
                 magnify(j, EVERY, K)
             magnify(j, EVERY, Q)
             take_root(j, EVERY, K)
-            if GS[j]:
-                take_shrink(j, EVERY, g, "G")
             if j in (1, 2, 3):
                 regroup_w((j + 4) // 2, "G", 2 if j % 2 else 0, 2)
+            if GS[j]:
+                take_shrink(j, EVERY, g, "G")
             take_root(j, EVERY, Q)
             add(j + 1, SETS, ALL)
             if j > 1:

@@ -108,10 +108,9 @@ def tile_decoder_pb_kernel(tc, hq1, hk1, proj1, bias1, out):
         def copy_bias(turned):
             nc.vector.tensor_copy(out=bias[:], in_=turned[:, 0 : HEADS * HALVES].bitcast(BF16))
 
-        def regroup_w(head, engine, first, count):
+        def regroup_w(head, engine, first, count, pool=ring):
             if (head, first) not in grouped_w:
-                pool = ring if engine == "G" else deep2
-                grouped_w[head, first] = pool.tile([P, count * P, PACK], BF16, align_bytes=64, name="grouped_w%s%d" % (engine, count))
+                grouped_w[head, first] = (pool if engine == "G" else deep2).tile([P, count * P, PACK], BF16, align_bytes=64, name="grouped_w%s%d" % (engine, count))
             grouped = grouped_w[head, first]
             columns = w_rows[head][:].rearrange("p t (u q e) -> p t u q e", q=P, e=PAIR)
             for m in range(first, first + count):
@@ -290,7 +289,7 @@ def tile_decoder_pb_kernel(tc, hq1, hk1, proj1, bias1, out):
             )
 
         GS = [0] + [P] * 3 + [SEQ] * 3 + [0]
-        XE = ["SV"] * 4 + ["SS"] * 4
+        XE = ["SV"] * 5 + ["SS"] * 3
         X2 = "SV"
         SE = "V"
         VT = "S"
@@ -299,16 +298,19 @@ def tile_decoder_pb_kernel(tc, hq1, hk1, proj1, bias1, out):
         LO, HI, EVERY = slice(0, 2), slice(2, 4), slice(0, 4)
         transpose_x(0, 0)
         bias_t = transpose_bias()
-        regroup_x(0, 0, "S")
-        regroup_w(0, "V", 0, 2)
-        copy_bias(bias_t)
+        regroup_w(0, "V", 0, 1)
+        regroup_w(0, "S", 1, 1)
+        regroup_x(0, 0, "V")
         regroup_w(0, "S", 2, 1)
+        quantise_w(0, 0, 1)
         quantise_x(0, Q)
-        quantise_w(0, 0, 2)
         transpose_x(0, 1)
-        project(0, (0, 1), Q)
-        regroup_x(0, 1, "S")
+        project(0, (0,), Q)
+        quantise_w(0, 1, 1)
+        project(0, (1,), Q)
         regroup_w(0, "V", 3, 1)
+        copy_bias(bias_t)
+        regroup_x(0, 1, "S")
         quantise_w(0, 2, 1)
         quantise_w(0, 3, 1)
         project(0, (2, 3), Q)

@@ -124,7 +124,7 @@ def tile_decoder_pb_kernel(tc, hq1, hk1, proj1, bias1, out):
                     if engine == "V":
                         nc.vector.tensor_copy(out=o, in_=s)
                     else:
-                        nc.scalar.copy(out=o, in_=s)
+                        nc.scalar.copy(out=target, in_=origin.rearrange("p t q -> p q t"))
 
         def quantise_w(head, first, count):
             if head not in w_codes:
@@ -289,7 +289,7 @@ def tile_decoder_pb_kernel(tc, hq1, hk1, proj1, bias1, out):
             )
 
         GS = [0] + [P] * 3 + [SEQ] * 3 + [0]
-        XE = ["SV"] * 5 + ["SS"] * 3
+        XE = ["SV"] * 4 + ["SS"] * 4
         X2 = "SV"
         SE = "V"
         VT = "S"
@@ -330,9 +330,9 @@ def tile_decoder_pb_kernel(tc, hq1, hk1, proj1, bias1, out):
         add(0, (1, 2, 3), K)
         project(1, SETS, ALL)
         take_root(0, EVERY, Q)
-        regroup_x(2, 0, X2[0])
         take_shrink(0, EVERY, Q)
         magnify(0, EVERY, K)
+        regroup_x(2, 0, X2[0])
         regroup_x(2, 1, X2[1])
         take_root(0, EVERY, K)
         add(1, SETS, ALL)
@@ -386,16 +386,17 @@ def tile_decoder_pb_kernel(tc, hq1, hk1, proj1, bias1, out):
         store(j - 2, K, "V")
         quantise_h(j - 1, ALL)
         score(j - 1, K)
-        magnify(j, EVERY, KB, VT)
-        take_shrink(j, EVERY, Q)
+        magnify(j, EVERY, KB)
+        take_shrink(j, EVERY, slice(0, P), "G")
+        take_shrink(j, EVERY, slice(P, SEQ))
         take_root(j, EVERY, KA)
         take_root(j, EVERY, KB)
         take_shrink(j, EVERY, KA)
         squash(j, Q)
-        store(j - 1, K, "V")
-        quantise_h(j, Q)
         take_shrink(j, EVERY, KB)
+        store(j - 1, K, "S")
         squash(j, KA)
+        quantise_h(j, Q)
         squash(j, KB)
         quantise_h(j, KA)
         score(j, KA)

from contextlib import ExitStack

import concourse.mybir as mybir
from concourse.masks import make_identity

BF16 = mybir.dt.bfloat16
F32 = mybir.dt.float32
U32 = mybir.dt.uint32
U8 = mybir.dt.uint8
FP8X4 = mybir.dt.float8_e4m3fn_x4
ACT = mybir.ActivationFunctionType
ALU = mybir.AluOpType

P = 128
PACK = 4
BATCH = 2
HEADS = 4
SEQ = 256
WIDTH = 512
GAMMA = 64.0
TOKEN_TILES = SEQ // P
FEATURE_TILES = WIDTH // P
PAIR = 2
HALVES = PACK // PAIR
SIDES = 2
TOKENS = SIDES * SEQ
PAIRS = HEADS * BATCH
HALF_WIDTH = WIDTH // HALVES
COPY_RUN = 4
WORD_RUN = 2

FLOPS = 2 * PAIRS * TOKENS * WIDTH * WIDTH + 2 * PAIRS * SEQ * SEQ * WIDTH

def tile_decoder_pb_kernel(tc, hq1, hk1, proj1, bias1, out):
    nc = tc.nc

    with ExitStack() as ctx:
        consts = ctx.enter_context(tc.tile_pool(name="consts", bufs=1))
        inputs = ctx.enter_context(tc.tile_pool(name="inputs", bufs=1))
        ring = ctx.enter_context(tc.tile_pool(name="ring", bufs=1))
        deep2 = ctx.enter_context(tc.tile_pool(name="deep2", bufs=2))
        deep3 = ctx.enter_context(tc.tile_pool(name="deep3", bufs=3))
        deep4 = ctx.enter_context(tc.tile_pool(name="deep4", bufs=4))
        psum_t = ctx.enter_context(tc.psum_pool(name="psum_t", bufs=2))
        psum_h = ctx.enter_context(tc.psum_pool(name="psum_h", bufs=4))
        psum_o = ctx.enter_context(tc.psum_pool(name="psum_o", bufs=2))
        ctx.enter_context(tc.manual_schedule())
        x_rows, w_rows, turned_x = {}, {}, {}
        grouped_x, x_codes, x_scales = {}, {}, {}
        grouped_w, w_codes, w_scales = {}, {}, {}
        acc, hidden, magnitude, root, shrink = {}, {}, {}, {}, {}
        grouped_h, h_codes, h_scales = {}, {}, {}
        scores = {}
        ALL = slice(0, TOKENS)
        Q = slice(0, SEQ)
        K = slice(SEQ, TOKENS)
        SETS = range(FEATURE_TILES)

        def load_x(pair, side):
            head, batch = pair // BATCH, pair % BATCH
            rows = inputs.tile([P, TOKEN_TILES, WIDTH], BF16, name="x_rows%d_%d" % (pair, side))
            source = (hq1, hk1)[side][batch, head]
            nc.sync.dma_start(out=rows[:], in_=source.rearrange("(a p) k -> p a k", p=P))
            x_rows[pair, side] = rows

        def load_w(head, halves):
            if head not in w_rows:
                w_rows[head] = inputs.tile([P, PACK, WIDTH], BF16, name="w_rows%d" % head)
            source = proj1[0, head].rearrange("(u p e) n -> p u e n", p=P, e=PAIR)
            target = w_rows[head][:].rearrange("p (u e) n -> p u e n", e=PAIR)
            if len(halves) == 2:
                nc.sync.dma_start(out=target, in_=source)
                return
            cols = slice(halves[0] * HALF_WIDTH, (halves[0] + 1) * HALF_WIDTH)
            for u in range(HALVES):
                nc.sync.dma_start(out=target[:, u, :, cols], in_=source[:, u, :, cols])

        load_x(0, 0)
        load_w(0, (0,))
        load_w(0, (1,))
        load_x(0, 1)
        for head in range(HEADS):
            if head > 0:
                load_w(head, (0, 1))
            for pair in range(max(1, head * BATCH), (head + 1) * BATCH):
                for side in range(SIDES):
                    load_x(pair, side)

        identity = consts.tile([P, P], F32)
        make_identity(nc, identity[:])
        bias_rows = consts.tile([P, PAIR * P], BF16)
        nc.vector.memset(bias_rows[:], 0.0)
        offset = consts.tile([P, 1], F32)
        nc.vector.memset(offset[:], 1.0 / GAMMA)
        nc.scalar.dma_start(
            out=bias_rows[0 : HEADS * HALVES, :],
            in_=bias1.rearrange("o h i (u w) -> (o h i u) w", u=HALVES),
        )
        bias = consts.tile([P, HEADS * FEATURE_TILES], F32)
        warm = consts.tile([P, 1], F32)
        nc.scalar.activation(out=warm[:], in_=offset[:], func=ACT.Abs_reciprocal_sqrt)

        def transpose_bias():
            turned = psum_o.tile([P, P], F32, name="product")
            nc.tensor.transpose(out=turned[:], in_=bias_rows[:].bitcast(F32), identity=identity[:])
            return turned

        def copy_bias(turned):
            nc.vector.tensor_copy(out=bias[:], in_=turned[:, 0 : HEADS * HALVES].bitcast(BF16))

        def regroup_w(head, engine, first, count, pool=ring):
            if (head, first) not in grouped_w:
                grouped_w[head, first] = (pool if engine == "G" else deep2).tile([P, count * P, PACK], BF16, align_bytes=64, name="grouped_w%s%d" % (engine, count))
            grouped = grouped_w[head, first]
            columns = w_rows[head][:].rearrange("p t (u q e) -> p t u q e", q=P, e=PAIR)
            for m in range(first, first + count):
                target = grouped[:, (m - first) * P : (m - first + 1) * P, :]
                origin = columns[:, :, m // PAIR, :, m % PAIR]
                if engine == "G":
                    nc.gpsimd.tensor_scalar(out=target, in0=origin.rearrange("p t q -> p q t"), scalar1=1.0, scalar2=0.0, op0=ALU.mult, op1=ALU.add)
                else:
                    o = target.rearrange("p (c i) t -> p c t i", i=COPY_RUN)
                    s = origin.rearrange("p t (c i) -> p c t i", i=COPY_RUN)
                    if engine == "V":
                        nc.vector.tensor_copy(out=o, in_=s)
                    else:
                        nc.scalar.copy(out=target, in_=origin.rearrange("p t q -> p q t"))

        def quantise_w(head, first, count):
            if head not in w_codes:
                w_codes[head] = deep2.tile([P, WIDTH], U32, align_bytes=64, name="w_codes")
                w_scales[head] = deep2.tile([P, WIDTH], U8, align_bytes=64, name="w_scales")
            cols = slice(first * P, (first + count) * P)
            nc.vector.quantize_mx(
                out=w_codes[head][:, cols].bitcast(FP8X4),
                scales=w_scales[head][:, cols],
                in_=grouped_w[head, first][:].rearrange("p n t -> p (n t)"),
            )

        def transpose_x(pair, side):
            if pair >= PAIRS:
                return
            turned = psum_t.tile([P, TOKEN_TILES, HALVES, P], F32, name="turned")
            for a in range(TOKEN_TILES):
                words = x_rows[pair, side][:, a, :].bitcast(F32)
                for u in range(HALVES):
                    nc.tensor.transpose(out=turned[:, a, u, :], in_=words[:, u * P : (u + 1) * P], identity=identity[:])
            turned_x[pair, side] = turned

        def regroup_x(pair, side, engine):
            if pair >= PAIRS:
                return
            if pair not in grouped_x:
                grouped_x[pair] = deep4.tile([P, TOKENS, PACK], BF16, align_bytes=64, name="grouped_x")
            words = grouped_x[pair][:].rearrange("p s t -> p (s t)").bitcast(F32)
            n = SEQ * HALVES
            target = words[:, side * n : (side + 1) * n].rearrange("p (a r u) -> p a r u", a=TOKEN_TILES, u=HALVES)
            origin = turned_x[pair, side][:].rearrange("p a u r -> p a r u")
            if engine == "S":
                nc.scalar.copy(out=target, in_=origin)
            else:
                nc.vector.tensor_copy(out=target, in_=origin)

        def quantise_x(pair, tok):
            if pair >= PAIRS:
                return
            if pair not in x_codes:
                x_codes[pair] = deep2.tile([P, TOKENS], U32, align_bytes=64, name="x_codes")
                x_scales[pair] = deep2.tile([P, TOKENS], U8, align_bytes=64, name="x_scales")
            nc.vector.quantize_mx(
                out=x_codes[pair][:, tok].bitcast(FP8X4),
                scales=x_scales[pair][:, tok],
                in_=grouped_x[pair][:, tok, :].rearrange("p s t -> p (s t)"),
            )

        def project(pair, ms, tok):
            if pair >= PAIRS:
                return
            head = pair // BATCH
            for m in ms:
                if (pair, m) not in acc:
                    acc[pair, m] = psum_h.tile([P, TOKENS], F32, name="sums")
                cols = slice(m * P, (m + 1) * P)
                nc.tensor.matmul_mx(
                    out=acc[pair, m][:, tok],
                    lhsT=w_codes[head][:, cols].bitcast(FP8X4),
                    lhsT_scale=w_scales[head][:, cols],
                    rhs=x_codes[pair][:, tok].bitcast(FP8X4),
                    rhs_scale=x_scales[pair][:, tok],
                    start=True,
                    stop=True,
                )

        def add(pair, ms, tok):
            if pair >= PAIRS:
                return
            if pair not in hidden:
                hidden[pair] = deep3.tile([P, FEATURE_TILES, TOKENS], F32, name="hidden")
                magnitude[pair] = deep2.tile([P, FEATURE_TILES, TOKENS], F32, name="magnitude")
                root[pair] = deep2.tile([P, FEATURE_TILES, TOKENS], F32, name="root")
                shrink[pair] = deep2.tile([P, FEATURE_TILES, TOKENS], F32, name="shrink")
            for m in ms:
                column = pair // BATCH * FEATURE_TILES + m
                nc.vector.scalar_tensor_tensor(
                    out=hidden[pair][:, m, tok],
                    in0=acc[pair, m][:, tok],
                    scalar=bias[:, column : column + 1],
                    in1=grouped_x[pair][:, tok, m],
                    op0=ALU.add,
                    op1=ALU.add,
                )

        def magnify(pair, ms, tok, engine="S"):
            h, a = hidden[pair][:, ms, tok], magnitude[pair][:, ms, tok]
            if engine == "S":
                nc.scalar.activation(out=a, in_=h, func=ACT.Abs)
            else:
                nc.vector.scalar_tensor_tensor(out=a, in0=h, scalar=-1.0, in1=h, op0=ALU.mult, op1=ALU.max)

        def take_root(pair, ms, tok):
            nc.scalar.activation(
                out=root[pair][:, ms, tok],
                in_=magnitude[pair][:, ms, tok],
                func=ACT.Abs_reciprocal_sqrt,
                bias=offset[:, 0:1],
            )

        def take_shrink(pair, ms, tok, engine="S"):
            r, s = root[pair][:, ms, tok], shrink[pair][:, ms, tok]
            if engine == "S":
                nc.scalar.activation(out=s, in_=r, func=ACT.Square)
            else:
                nc.gpsimd.tensor_tensor(out=s, in0=r, in1=r, op=ALU.mult)

        def squash(pair, tok):
            if pair < 0:
                return
            if pair not in grouped_h:
                grouped_h[pair] = deep2.tile([P, TOKENS, PACK], BF16, align_bytes=64, name="grouped_h")
                h_codes[pair] = deep2.tile([P, TOKENS], U32, align_bytes=64, name="h_codes")
                h_scales[pair] = deep2.tile([P, TOKENS], U8, align_bytes=64, name="h_scales")
            nc.vector.tensor_tensor(
                out=grouped_h[pair][:, tok, :].rearrange("p (c i) t -> p c t i", i=WORD_RUN),
                in0=hidden[pair][:, :, tok].rearrange("p t (c i) -> p c t i", i=WORD_RUN),
                in1=shrink[pair][:, :, tok].rearrange("p t (c i) -> p c t i", i=WORD_RUN),
                op=ALU.mult,
            )

        def quantise_h(pair, tok):
            if pair < 0:
                return
            nc.vector.quantize_mx(
                out=h_codes[pair][:, tok].bitcast(FP8X4),
                scales=h_scales[pair][:, tok],
                in_=grouped_h[pair][:, tok, :].rearrange("p s t -> p (s t)"),
            )

        def score(pair, keys):
            if pair < 0:
                return
            n = keys.stop - keys.start
            product = psum_o.tile([P, TOKEN_TILES, n], F32, name="product")
            for a in range(TOKEN_TILES):
                cols = slice(a * P, (a + 1) * P)
                nc.tensor.matmul_mx(
                    out=product[:, a, :],
                    lhsT=h_codes[pair][:, cols].bitcast(FP8X4),
                    lhsT_scale=h_scales[pair][:, cols],
                    rhs=h_codes[pair][:, keys].bitcast(FP8X4),
                    rhs_scale=h_scales[pair][:, keys],
                    start=True,
                    stop=True,
                )
            scores[pair, keys.start] = product

        def store(pair, keys, engine):
            if pair < 0:
                return
            head, batch = pair // BATCH, pair % BATCH
            n = keys.stop - keys.start
            result = deep2.tile([P, TOKEN_TILES, n], F32, name="result%d" % n)
            if engine == "S":
                nc.scalar.copy(out=result[:], in_=scores[pair, keys.start][:])
            else:
                nc.vector.tensor_copy(out=result[:], in_=scores[pair, keys.start][:])
            nc.sync.dma_start(
                out=out[batch, head].rearrange("(a p) t -> p a t", p=P)[:, :, keys.start - SEQ : keys.stop - SEQ],
                in_=result[:],
            )

        GS = [0] + [P] * 3 + [SEQ] * 3 + [0]
        XE = ["SV"] * 4 + ["SS"] * 4
        X2 = "SV"
        SE = "V"
        VT = "S"


        LO, HI, EVERY = slice(0, 2), slice(2, 4), slice(0, 4)
        transpose_x(0, 0)
        bias_t = transpose_bias()
        regroup_w(0, "V", 0, 1)
        regroup_w(0, "S", 1, 1)
        regroup_x(0, 0, "V")
        regroup_w(0, "S", 2, 1)
        quantise_w(0, 0, 1)
        quantise_x(0, Q)
        transpose_x(0, 1)
        project(0, (0,), Q)
        quantise_w(0, 1, 1)
        project(0, (1,), Q)
        regroup_w(0, "V", 3, 1)
        copy_bias(bias_t)
        regroup_x(0, 1, "S")
        quantise_w(0, 2, 1)
        quantise_w(0, 3, 1)
        project(0, (2, 3), Q)
        transpose_x(1, 0)
        add(0, SETS, Q)
        magnify(0, LO, Q)
        magnify(0, HI, Q)
        quantise_x(0, K)
        transpose_x(1, 1)
        project(0, SETS, K)
        regroup_x(1, 0, "V")
        regroup_x(1, 1, "V")
        transpose_x(2, 0)
        transpose_x(2, 1)
        add(0, (0,), K)
        quantise_x(1, ALL)
        add(0, (1, 2, 3), K)
        project(1, SETS, ALL)
        take_root(0, EVERY, Q)
        take_shrink(0, EVERY, Q)
        magnify(0, EVERY, K)
        regroup_x(2, 0, X2[0])
        regroup_x(2, 1, X2[1])
        take_root(0, EVERY, K)
        add(1, SETS, ALL)
        magnify(1, EVERY, K)
        take_shrink(0, EVERY, K)
        regroup_w(1, "V", 0, 2)
        regroup_w(1, "V", 2, 2)
        quantise_w(1, 0, 2)
        quantise_x(2, ALL)
        quantise_w(1, 2, 2)
        transpose_x(3, 0)
        transpose_x(3, 1)
        project(2, SETS, ALL)
        regroup_w(2, "G", 0, 2)

        def gsplit(j):
            return slice(0, TOKENS - GS[j]), slice(TOKENS - GS[j], TOKENS)
        for j in range(1, PAIRS - 1):
            s, g = gsplit(j)
            if j in (1, 2, 3, 4):
                quantise_w(j // 2 + 1 if j % 2 == 0 else (j + 3) // 2, 0 if j % 2 else 2, 2)
            squash(j - 1, ALL)
            if j > 1:
                magnify(j, EVERY, K)
            magnify(j, EVERY, Q)
            take_root(j, EVERY, K)
            if j in (1, 2, 3):
                regroup_w((j + 4) // 2, "G", 2 if j % 2 else 0, 2)
            if GS[j]:
                take_shrink(j, EVERY, g, "G")
            take_root(j, EVERY, Q)
            add(j + 1, SETS, ALL)
            if j > 1:
                store(j - 2, K, SE)
            regroup_x(j + 2, 0, XE[j][0])
            regroup_x(j + 2, 1, XE[j][1])
            take_shrink(j, EVERY, s)
            quantise_h(j - 1, ALL)
            score(j - 1, K)
            quantise_x(j + 2, ALL)
            transpose_x(j + 3, 0)
            transpose_x(j + 3, 1)
            project(j + 2, SETS, ALL)

        j = PAIRS - 1
        KA, KB = slice(SEQ, SEQ + P), slice(SEQ + P, TOKENS)
        squash(j - 1, ALL)
        magnify(j, EVERY, Q)
        magnify(j, EVERY, KA)
        take_root(j, EVERY, Q)
        store(j - 2, K, "V")
        quantise_h(j - 1, ALL)
        score(j - 1, K)
        magnify(j, EVERY, KB)
        take_shrink(j, EVERY, slice(0, P), "G")
        take_shrink(j, EVERY, slice(P, SEQ))
        take_root(j, EVERY, KA)
        take_root(j, EVERY, KB)
        take_shrink(j, EVERY, KA)
        squash(j, Q)
        take_shrink(j, EVERY, KB)
        store(j - 1, K, "S")
        squash(j, KA)
        quantise_h(j, Q)
        squash(j, KB)
        quantise_h(j, KA)
        score(j, KA)
        quantise_h(j, KB)
        score(j, KB)
        store(j, KA, "V")
        store(j, KB, "V")
